import numpy as np
import ml_dtypes


def mxq(x, axis, fmt="e4m3"):
    dtype, down = {"e4m3": (ml_dtypes.float8_e4m3fn, 7), "e5m2": (ml_dtypes.float8_e5m2, 14)}[fmt]
    v = np.moveaxis(np.asarray(x, np.float32).astype(ml_dtypes.bfloat16).astype(np.float64), axis, -1)
    blocks = v.reshape(v.shape[:-1] + (-1, 32))
    amax = np.abs(blocks).max(-1, keepdims=True)
    byte = np.maximum(np.where(amax > 0, np.frexp(amax)[1] - 1 + 127, 0) - down, 1)
    scale = np.exp2(byte - 127.0)
    codes = (blocks / scale).astype(np.float32).astype(dtype).astype(np.float64)
    return np.moveaxis((codes * scale).reshape(v.shape), -1, axis)


WIDE = False


def mx_kscale(k):
    if not WIDE:
        return np.ones(k)
    levels = np.array([10, -10, 5, -5, 0])
    a = np.random.permutation(np.resize(levels, k // 512 * 4)).reshape(k // 512, 4)
    idx = np.arange(k)
    return np.exp2(a[idx // 512, idx % 128 // 32])


BF16 = ml_dtypes.bfloat16


def bf(x):
    return np.asarray(x, np.float32).astype(BF16)


def f64(x):
    return np.asarray(x).astype(np.float64)


B, N, IN_DIM, OUT_DIM, H = 1, 2048, 512, 512, 4
HEAD_DIM = OUT_DIM // H
EDGE_P = 0.01


def setup_inputs():
    s = mx_kscale(IN_DIM)
    adj = np.maximum((np.random.random((N, N)) < EDGE_P) * 1.0, np.eye(N))
    return {"q": bf(np.random.standard_normal((B, H, N, HEAD_DIM))),
            "k": bf(np.random.standard_normal((B, H, N, HEAD_DIM))),
            "h": bf(np.random.standard_normal((B, N, IN_DIM)) * s),
            "w_v": bf(np.random.standard_normal((IN_DIM, OUT_DIM)) / np.sqrt(IN_DIM) / s[:, None]),
            "adj": bf(adj)}


def reference(q, k, h, w_v, adj):
    v = mxq(f64(h), 2, "e4m3") @ mxq(f64(w_v), 0, "e4m3")
    v = v.reshape(B, N, H, HEAD_DIM).transpose(0, 2, 1, 3)
    mask = np.where(f64(adj) == 0, -np.inf, 0.0)
    s = f64(q) @ f64(k).transpose(0, 1, 3, 2) / np.sqrt(HEAD_DIM) + mask
    e = np.exp(s - s.max(-1, keepdims=True))
    out = (mxq(e, 3, "e4m3") @ mxq(v, 2, "e4m3")) / e.sum(-1, keepdims=True)
    return out.transpose(0, 2, 1, 3).reshape(B, N, OUT_DIM)

@@ -1,0 +1,268 @@
+import math
+from contextlib import ExitStack
+
+import concourse.mybir as mybir
+from concourse.masks import make_identity
+
+FLOPS = 2 * 2048 * 512 * 512 + 2 * (2 * 4 * 2048 * 2048 * 128)
+
+FP8X4 = mybir.dt.float8_e4m3fn_x4
+BF16 = mybir.dt.bfloat16
+F32 = mybir.dt.float32
+U32 = mybir.dt.uint32
+U8 = mybir.dt.uint8
+ALU = mybir.AluOpType
+ACT = mybir.ActivationFunctionType
+AXIS = mybir.AxisListType
+
+P = 128
+PACK = 4
+K_PASS = P * PACK
+BANK = 512
+NODES = 2048
+FEATURES = 512
+HEADS = 4
+HEAD_DIM = 128
+ROW_TILES = NODES // P
+UNITS = ROW_TILES * HEADS
+SCORE_BANKS = NODES // BANK
+NODE_PASSES = NODES // K_PASS
+SCALE = 1.0 / math.sqrt(HEAD_DIM)
+HUGE = 3.0e38
+
+
+def cols(index, width):
+    return slice(index * width, (index + 1) * width)
+
+
+def tile_gatlayer_pa_kernel(tc, q, k, h, w_v, adj, out):
+    nc = tc.nc
+    with ExitStack() as ctx:
+        const = ctx.enter_context(tc.tile_pool(name="const", bufs=1))
+        keep = ctx.enter_context(tc.tile_pool(name="keep", bufs=1))
+        stage = ctx.enter_context(tc.tile_pool(name="stage", bufs=2))
+        rows = ctx.enter_context(tc.tile_pool(name="rows", bufs=2))
+        work = ctx.enter_context(tc.tile_pool(name="work", bufs=3))
+        ps_prod = ctx.enter_context(tc.psum_pool(name="ps_prod", bufs=4))
+        ps_flip = ctx.enter_context(tc.psum_pool(name="ps_flip", bufs=2))
+        ps_out = ctx.enter_context(tc.psum_pool(name="ps_out", bufs=2))
+
+        ident_f32 = const.tile([P, P], F32)
+        make_identity(nc, ident_f32[:])
+        ident_bf16 = const.tile([P, P], BF16)
+        make_identity(nc, ident_bf16[:])
+
+        def copy_out(piece, out_ap, in_ap):
+            if piece % 2 == 0:
+                nc.vector.tensor_copy(out=out_ap, in_=in_ap)
+            else:
+                nc.scalar.copy(out=out_ap, in_=in_ap)
+
+        w_rows = stage.tile([P, PACK, FEATURES], BF16)
+        nc.sync.dma_start(
+            out=w_rows[:].rearrange("p (u b) c -> p u b c", u=2),
+            in_=w_v.rearrange("(u p b) c -> p u b c", u=2, b=2),
+        )
+        w_grouped = stage.tile([P, FEATURES * PACK], BF16, align_bytes=64)
+        nc.vector.tensor_copy(
+            out=w_grouped[:].rearrange("p (c t) -> p c t", t=PACK),
+            in_=w_rows[:].rearrange("p t c -> p c t"),
+        )
+        w_codes = keep.tile([P, FEATURES], U32, align_bytes=64)
+        w_scales = keep.tile([P, FEATURES], U8, align_bytes=64)
+        nc.vector.quantize_mx(out=w_codes[:].bitcast(FP8X4), scales=w_scales[:], in_=w_grouped[:])
+
+        h_codes = keep.tile([P, NODES], U32, align_bytes=64)
+        h_scales = keep.tile([P, NODES], U8, align_bytes=64)
+        for a in range(NODES // (2 * P)):
+            h_rows = stage.tile([P, 2, FEATURES], BF16)
+            nc.sync.dma_start(
+                out=h_rows[:],
+                in_=h[0, cols(a, 2 * P), :].rearrange("(p b) k -> p b k", b=2),
+            )
+            h_flip = ps_flip.tile([P, BANK], F32, tag="flip")
+            for b in range(2):
+                h_pairs = h_rows[:, b, :].bitcast(F32)
+                for u in range(2):
+                    nc.tensor.transpose(h_flip[:, cols(2 * b + u, P)], h_pairs[:, cols(u, P)], ident_f32[:])
+            h_grouped = stage.tile([P, 2 * P * PACK], BF16, align_bytes=64)
+            copy_out(
+                a,
+                h_grouped[:].bitcast(F32).rearrange("p (b r u) -> p b r u", b=2, u=2),
+                h_flip[:].rearrange("p (b u r) -> p b r u", b=2, u=2),
+            )
+            nc.vector.quantize_mx(
+                out=h_codes[:, cols(a, 2 * P)].bitcast(FP8X4),
+                scales=h_scales[:, cols(a, 2 * P)],
+                in_=h_grouped[:],
+            )
+
+        v_codes = keep.tile([P, NODE_PASSES, FEATURES], U32, align_bytes=64)
+        v_scales = keep.tile([P, NODE_PASSES, FEATURES], U8, align_bytes=64)
+        for g in range(NODE_PASSES):
+            v_rows = stage.tile([P, PACK, FEATURES], BF16)
+            for t in range(PACK):
+                v_sum = ps_prod.tile([P, BANK], F32, tag="prod")
+                nc.tensor.matmul_mx(
+                    out=v_sum[:],
+                    lhsT=h_codes[:, cols(PACK * g + t, P)].bitcast(FP8X4),
+                    lhsT_scale=h_scales[:, cols(PACK * g + t, P)],
+                    rhs=w_codes[:].bitcast(FP8X4),
+                    rhs_scale=w_scales[:],
+                    start=True,
+                    stop=True,
+                )
+                copy_out(t, v_rows[:, t, :], v_sum[:])
+            v_grouped = stage.tile([P, FEATURES * PACK], BF16, align_bytes=64)
+            nc.vector.tensor_copy(
+                out=v_grouped[:].rearrange("p (c t) -> p c t", t=PACK),
+                in_=v_rows[:].rearrange("p t c -> p c t"),
+            )
+            nc.vector.quantize_mx(
+                out=v_codes[:, g, :].bitcast(FP8X4), scales=v_scales[:, g, :], in_=v_grouped[:]
+            )
+
+        k_flipped = keep.tile([P, HEADS, NODES], BF16)
+        for head in range(HEADS):
+            k_rows = stage.tile([P, ROW_TILES, HEAD_DIM], BF16)
+            nc.sync.dma_start(out=k_rows[:], in_=k[0, head].rearrange("(t p) d -> p t d", p=P))
+            for c in range(SCORE_BANKS):
+                k_flip = ps_flip.tile([P, BANK], BF16, tag="flip")
+                for t in range(BANK // P):
+                    nc.tensor.transpose(k_flip[:, cols(t, P)], k_rows[:, (BANK // P) * c + t, :], ident_bf16[:])
+                copy_out(c, k_flipped[:, head, cols(c, BANK)], k_flip[:])
+
+        q_rows = {}
+        q_flipped = {}
+        penalty = {}
+        row_sum = {}
+        out_sum = {}
+        scores = {}
+        neg_scores = {}
+        neg_max = {}
+        e_grouped = {}
+
+        def load_rows(i):
+            q_tile = rows.tile([P, HEADS, HEAD_DIM], BF16)
+            nc.sync.dma_start(out=q_tile[:], in_=q[0, :, cols(i, P), :].rearrange("n p d -> p n d"))
+            q_rows[i] = q_tile
+            pen = rows.tile([P, NODES], BF16)
+            nc.sync.dma_start(out=pen[:], in_=adj[cols(i, P), :])
+            nc.gpsimd.tensor_scalar(
+                out=pen[:], in0=pen[:], scalar1=-HUGE, scalar2=HUGE, op0=ALU.mult, op1=ALU.add
+            )
+            penalty[i] = pen
+
+        def flip_queries(i):
+            q_flip = ps_flip.tile([P, BANK], BF16, tag="flip")
+            for head in range(HEADS):
+                nc.tensor.transpose(q_flip[:, cols(head, P)], q_rows[i][:, head, :], ident_bf16[:])
+            q_t = rows.tile([P, HEADS * P], BF16)
+            nc.scalar.copy(out=q_t[:], in_=q_flip[:])
+            q_flipped[i] = q_t
+
+        def score_matmul(unit, c):
+            i, head = divmod(unit, HEADS)
+            s_bank = ps_prod.tile([P, BANK], F32, tag="prod")
+            nc.tensor.matmul(
+                out=s_bank[:],
+                lhsT=q_flipped[i][:, cols(head, P)],
+                rhs=k_flipped[:, head, cols(c, BANK)],
+                start=True,
+                stop=True,
+            )
+            scores[(unit, c)] = s_bank
+
+        def mask_and_minimum(unit):
+            i = unit // HEADS
+            x = work.tile([P, NODES], F32)
+            for c in range(SCORE_BANKS):
+                nc.vector.scalar_tensor_tensor(
+                    out=x[:, cols(c, BANK)],
+                    in0=scores[(unit, c)][:],
+                    scalar=-SCALE,
+                    in1=penalty[i][:, cols(c, BANK)],
+                    op0=ALU.mult,
+                    op1=ALU.add,
+                )
+                if unit + 1 < UNITS:
+                    score_matmul(unit + 1, c)
+            x_min = work.tile([P, 1], F32)
+            nc.vector.tensor_reduce(out=x_min[:], in_=x[:], axis=AXIS.X, op=ALU.min)
+            neg_scores[unit] = x
+            neg_max[unit] = x_min
+
+        def exponentials_flipped(unit):
+            i, head = divmod(unit, HEADS)
+            if head == 0:
+                sums = rows.tile([P, HEADS], F32)
+                row_sum[i] = sums
+            e = work.tile([P, NODES], BF16)
+            nc.scalar.activation(
+                out=e[:],
+                in_=neg_scores[unit][:],
+                func=ACT.Exp,
+                bias=neg_max[unit][:],
+                scale=-1.0,
+                accum_out=row_sum[i][:, head : head + 1],
+            )
+            e_pairs = e[:].bitcast(F32)
+            grouped = work.tile([P, NODE_PASSES * P * PACK], BF16, align_bytes=64)
+            grouped_pairs = grouped[:].bitcast(F32).rearrange("p (g r u) -> p g r u", r=P, u=2)
+            for half in range(2):
+                e_flip = ps_flip.tile([P, BANK], F32, tag="flip")
+                for t in range(4):
+                    nc.tensor.transpose(e_flip[:, cols(t, P)], e_pairs[:, cols(4 * half + t, P)], ident_f32[:])
+                nc.scalar.copy(
+                    out=grouped_pairs[:, cols(half, 2), :, :],
+                    in_=e_flip[:].rearrange("p (g u r) -> p g r u", g=2, u=2),
+                )
+            e_grouped[unit] = grouped
+
+        def quantise_and_aggregate(unit):
+            i, head = divmod(unit, HEADS)
+            e_codes = work.tile([P, NODE_PASSES * P], U32, align_bytes=64)
+            e_scales = work.tile([P, NODE_PASSES * P], U8, align_bytes=64)
+            nc.vector.quantize_mx(out=e_codes[:].bitcast(FP8X4), scales=e_scales[:], in_=e_grouped[unit][:])
+            if head == 0:
+                o_bank = ps_out.tile([P, BANK], F32, tag="out")
+                out_sum[i] = o_bank
+            for g in range(NODE_PASSES):
+                nc.tensor.matmul_mx(
+                    out=out_sum[i][:, cols(head, HEAD_DIM)],
+                    lhsT=e_codes[:, cols(g, P)].bitcast(FP8X4),
+                    lhsT_scale=e_scales[:, cols(g, P)],
+                    rhs=v_codes[:, g, cols(head, HEAD_DIM)].bitcast(FP8X4),
+                    rhs_scale=v_scales[:, g, cols(head, HEAD_DIM)],
+                    start=(g == 0),
+                    stop=(g == NODE_PASSES - 1),
+                )
+            if head == HEADS - 1:
+                inverse = rows.tile([P, HEADS], F32)
+                nc.vector.reciprocal(out=inverse[:], in_=row_sum[i][:])
+                result = rows.tile([P, FEATURES], F32)
+                for n in range(HEADS):
+                    nc.scalar.activation(
+                        out=result[:, cols(n, HEAD_DIM)],
+                        in_=out_sum[i][:, cols(n, HEAD_DIM)],
+                        func=ACT.Copy,
+                        scale=inverse[:, n : n + 1],
+                    )
+                nc.sync.dma_start(out=out[0, cols(i, P), :], in_=result[:])
+
+        load_rows(0)
+        flip_queries(0)
+        for c in range(SCORE_BANKS):
+            score_matmul(0, c)
+        for unit in range(UNITS + 1):
+            i, head = divmod(unit, HEADS)
+            if head == 0 and i + 1 < ROW_TILES:
+                load_rows(i + 1)
+            if unit >= 1:
+                exponentials_flipped(unit - 1)
+            if head == 2 and i + 1 < ROW_TILES:
+                flip_queries(i + 1)
+            if unit < UNITS:
+                mask_and_minimum(unit)
+            if unit >= 1:
+                quantise_and_aggregate(unit - 1)

@@ -52,95 +52,18 @@ def tile_gatlayer_pa_kernel(tc, q, k, h, w_v, adj, out):
         ident_bf16 = const.tile([P, P], BF16)
         make_identity(nc, ident_bf16[:])
 
-        def copy_out(piece, out_ap, in_ap):
-            if piece % 2 == 0:
-                nc.vector.tensor_copy(out=out_ap, in_=in_ap)
-            else:
-                nc.scalar.copy(out=out_ap, in_=in_ap)
-
-        w_rows = stage.tile([P, PACK, FEATURES], BF16)
-        nc.sync.dma_start(
-            out=w_rows[:].rearrange("p (u b) c -> p u b c", u=2),
-            in_=w_v.rearrange("(u p b) c -> p u b c", u=2, b=2),
-        )
-        w_grouped = stage.tile([P, FEATURES * PACK], BF16, align_bytes=64)
-        nc.vector.tensor_copy(
-            out=w_grouped[:].rearrange("p (c t) -> p c t", t=PACK),
-            in_=w_rows[:].rearrange("p t c -> p c t"),
-        )
-        w_codes = keep.tile([P, FEATURES], U32, align_bytes=64)
-        w_scales = keep.tile([P, FEATURES], U8, align_bytes=64)
-        nc.vector.quantize_mx(out=w_codes[:].bitcast(FP8X4), scales=w_scales[:], in_=w_grouped[:])
-
-        h_codes = keep.tile([P, NODES], U32, align_bytes=64)
-        h_scales = keep.tile([P, NODES], U8, align_bytes=64)
-        for a in range(NODES // (2 * P)):
-            h_rows = stage.tile([P, 2, FEATURES], BF16)
-            nc.sync.dma_start(
-                out=h_rows[:],
-                in_=h[0, cols(a, 2 * P), :].rearrange("(p b) k -> p b k", b=2),
+        def regroup(grouped, by_row):
+            nc.gpsimd.tensor_scalar(
+                out=grouped[:].rearrange("p (c t) -> p c t", t=PACK),
+                in0=by_row[:].rearrange("p t c -> p c t"),
+                scalar1=1.0,
+                scalar2=0.0,
+                op0=ALU.mult,
+                op1=ALU.add,
             )
-            h_flip = ps_flip.tile([P, BANK], F32, tag="flip")
-            for b in range(2):
-                h_pairs = h_rows[:, b, :].bitcast(F32)
-                for u in range(2):
-                    nc.tensor.transpose(h_flip[:, cols(2 * b + u, P)], h_pairs[:, cols(u, P)], ident_f32[:])
-            h_grouped = stage.tile([P, 2 * P * PACK], BF16, align_bytes=64)
-            copy_out(
-                a,
-                h_grouped[:].bitcast(F32).rearrange("p (b r u) -> p b r u", b=2, u=2),
-                h_flip[:].rearrange("p (b u r) -> p b r u", b=2, u=2),
-            )
-            nc.vector.quantize_mx(
-                out=h_codes[:, cols(a, 2 * P)].bitcast(FP8X4),
-                scales=h_scales[:, cols(a, 2 * P)],
-                in_=h_grouped[:],
-            )
-
-        v_codes = keep.tile([P, NODE_PASSES, FEATURES], U32, align_bytes=64)
-        v_scales = keep.tile([P, NODE_PASSES, FEATURES], U8, align_bytes=64)
-        for g in range(NODE_PASSES):
-            v_rows = stage.tile([P, PACK, FEATURES], BF16)
-            for t in range(PACK):
-                v_sum = ps_prod.tile([P, BANK], F32, tag="prod")
-                nc.tensor.matmul_mx(
-                    out=v_sum[:],
-                    lhsT=h_codes[:, cols(PACK * g + t, P)].bitcast(FP8X4),
-                    lhsT_scale=h_scales[:, cols(PACK * g + t, P)],
-                    rhs=w_codes[:].bitcast(FP8X4),
-                    rhs_scale=w_scales[:],
-                    start=True,
-                    stop=True,
-                )
-                copy_out(t, v_rows[:, t, :], v_sum[:])
-            v_grouped = stage.tile([P, FEATURES * PACK], BF16, align_bytes=64)
-            nc.vector.tensor_copy(
-                out=v_grouped[:].rearrange("p (c t) -> p c t", t=PACK),
-                in_=v_rows[:].rearrange("p t c -> p c t"),
-            )
-            nc.vector.quantize_mx(
-                out=v_codes[:, g, :].bitcast(FP8X4), scales=v_scales[:, g, :], in_=v_grouped[:]
-            )
-
-        k_flipped = keep.tile([P, HEADS, NODES], BF16)
-        for head in range(HEADS):
-            k_rows = stage.tile([P, ROW_TILES, HEAD_DIM], BF16)
-            nc.sync.dma_start(out=k_rows[:], in_=k[0, head].rearrange("(t p) d -> p t d", p=P))
-            for c in range(SCORE_BANKS):
-                k_flip = ps_flip.tile([P, BANK], BF16, tag="flip")
-                for t in range(BANK // P):
-                    nc.tensor.transpose(k_flip[:, cols(t, P)], k_rows[:, (BANK // P) * c + t, :], ident_bf16[:])
-                copy_out(c, k_flipped[:, head, cols(c, BANK)], k_flip[:])
 
         q_rows = {}
-        q_flipped = {}
         penalty = {}
-        row_sum = {}
-        out_sum = {}
-        scores = {}
-        neg_scores = {}
-        neg_max = {}
-        e_grouped = {}
 
         def load_rows(i):
             q_tile = rows.tile([P, HEADS, HEAD_DIM], BF16)
@@ -148,10 +71,106 @@ def tile_gatlayer_pa_kernel(tc, q, k, h, w_v, adj, out):
             q_rows[i] = q_tile
             pen = rows.tile([P, NODES], BF16)
             nc.sync.dma_start(out=pen[:], in_=adj[cols(i, P), :])
-            nc.gpsimd.tensor_scalar(
-                out=pen[:], in0=pen[:], scalar1=-HUGE, scalar2=HUGE, op0=ALU.mult, op1=ALU.add
-            )
             penalty[i] = pen
+
+        k_rows = keep.tile([P, HEADS, ROW_TILES, HEAD_DIM], BF16)
+
+        def load_keys(head):
+            nc.sync.dma_start(out=k_rows[:, head, :, :], in_=k[0, head].rearrange("(t p) d -> p t d", p=P))
+
+        load_keys(0)
+        load_rows(0)
+        load_keys(1)
+        w_rows = keep.tile([P, PACK, FEATURES], BF16)
+        nc.sync.dma_start(
+            out=w_rows[:].rearrange("p (u b) c -> p u b c", u=2),
+            in_=w_v.rearrange("(u p b) c -> p u b c", u=2, b=2),
+        )
+        h_rows = keep.tile([P, NODES // (2 * P), 2, FEATURES], BF16)
+        for g in range(NODE_PASSES):
+            nc.sync.dma_start(
+                out=h_rows[:, cols(g, 2), :, :],
+                in_=h[0, cols(g, K_PASS), :].rearrange("(a p b) k -> p a b k", a=2, b=2),
+            )
+        load_keys(2)
+        load_keys(3)
+
+        w_codes = keep.tile([P, FEATURES], U32, align_bytes=64)
+        w_scales = keep.tile([P, FEATURES], U8, align_bytes=64)
+        h_codes = keep.tile([P, NODES], U32, align_bytes=64)
+        h_scales = keep.tile([P, NODES], U8, align_bytes=64)
+        v_codes = keep.tile([P, NODE_PASSES, FEATURES], U32, align_bytes=64)
+        v_scales = keep.tile([P, NODE_PASSES, FEATURES], U8, align_bytes=64)
+
+        def project_values():
+            w_grouped = stage.tile([P, FEATURES * PACK], BF16, align_bytes=64)
+            regroup(w_grouped, w_rows)
+            nc.vector.quantize_mx(out=w_codes[:].bitcast(FP8X4), scales=w_scales[:], in_=w_grouped[:])
+
+            for a in range(NODES // (2 * P)):
+                h_flip = ps_flip.tile([P, BANK], F32, tag="flip")
+                for b in range(2):
+                    h_pairs = h_rows[:, a, b, :].bitcast(F32)
+                    for u in range(2):
+                        nc.tensor.transpose(h_flip[:, cols(2 * b + u, P)], h_pairs[:, cols(u, P)], ident_f32[:])
+                h_grouped = stage.tile([P, 2 * P * PACK], BF16, align_bytes=64)
+                nc.scalar.copy(
+                    out=h_grouped[:].bitcast(F32).rearrange("p (b r u) -> p b r u", b=2, u=2),
+                    in_=h_flip[:].rearrange("p (b u r) -> p b r u", b=2, u=2),
+                )
+                nc.vector.quantize_mx(
+                    out=h_codes[:, cols(a, 2 * P)].bitcast(FP8X4),
+                    scales=h_scales[:, cols(a, 2 * P)],
+                    in_=h_grouped[:],
+                )
+
+            for g in range(NODE_PASSES):
+                v_rows = stage.tile([P, PACK, FEATURES], BF16)
+                for t in range(PACK):
+                    v_sum = ps_out.tile([P, BANK], F32, tag="out")
+                    nc.tensor.matmul_mx(
+                        out=v_sum[:],
+                        lhsT=h_codes[:, cols(PACK * g + t, P)].bitcast(FP8X4),
+                        lhsT_scale=h_scales[:, cols(PACK * g + t, P)],
+                        rhs=w_codes[:].bitcast(FP8X4),
+                        rhs_scale=w_scales[:],
+                        start=True,
+                        stop=True,
+                    )
+                    nc.scalar.copy(out=v_rows[:, t, :], in_=v_sum[:])
+                v_grouped = stage.tile([P, FEATURES * PACK], BF16, align_bytes=64)
+                regroup(v_grouped, v_rows)
+                nc.vector.quantize_mx(
+                    out=v_codes[:, g, :].bitcast(FP8X4), scales=v_scales[:, g, :], in_=v_grouped[:]
+                )
+
+        k_flipped = keep.tile([P, HEADS, NODES], BF16)
+
+        def flip_keys(head):
+            for c in range(SCORE_BANKS):
+                k_flip = ps_flip.tile([P, BANK], BF16, tag="flip")
+                for t in range(BANK // P):
+                    nc.tensor.transpose(k_flip[:, cols(t, P)], k_rows[:, head, (BANK // P) * c + t, :], ident_bf16[:])
+                nc.scalar.copy(out=k_flipped[:, head, cols(c, BANK)], in_=k_flip[:])
+
+        q_flipped = {}
+        row_sum = {}
+        out_sum = {}
+        scores = {}
+        neg_scores = {}
+        neg_max = {}
+        weights = {}
+        e_grouped = {}
+
+        def make_penalty(i):
+            nc.gpsimd.tensor_scalar(
+                out=penalty[i][:],
+                in0=penalty[i][:],
+                scalar1=-HUGE,
+                scalar2=HUGE,
+                op0=ALU.mult,
+                op1=ALU.add,
+            )
 
         def flip_queries(i):
             q_flip = ps_flip.tile([P, BANK], BF16, tag="flip")
@@ -173,10 +192,19 @@ def tile_gatlayer_pa_kernel(tc, q, k, h, w_v, adj, out):
             )
             scores[(unit, c)] = s_bank
 
-        def mask_and_minimum(unit):
+        def mask_by_scalar_and_gpsimd(unit):
             i = unit // HEADS
             x = work.tile([P, NODES], F32)
-            for c in range(SCORE_BANKS):
+            neg_scores[unit] = x
+            nc.scalar.activation(out=x[:, cols(0, BANK)], in_=scores[(unit, 0)][:], func=ACT.Copy, scale=-SCALE)
+            nc.gpsimd.tensor_tensor(
+                out=x[:, cols(0, BANK)], in0=x[:, cols(0, BANK)], in1=penalty[i][:, cols(0, BANK)], op=ALU.add
+            )
+
+        def mask_by_vector_and_minimum(unit):
+            i = unit // HEADS
+            x = neg_scores[unit]
+            for c in range(1, SCORE_BANKS):
                 nc.vector.scalar_tensor_tensor(
                     out=x[:, cols(c, BANK)],
                     in0=scores[(unit, c)][:],
@@ -189,10 +217,9 @@ def tile_gatlayer_pa_kernel(tc, q, k, h, w_v, adj, out):
                     score_matmul(unit + 1, c)
             x_min = work.tile([P, 1], F32)
             nc.vector.tensor_reduce(out=x_min[:], in_=x[:], axis=AXIS.X, op=ALU.min)
-            neg_scores[unit] = x
             neg_max[unit] = x_min
 
-        def exponentials_flipped(unit):
+        def exponentials(unit):
             i, head = divmod(unit, HEADS)
             if head == 0:
                 sums = rows.tile([P, HEADS], F32)
@@ -206,7 +233,10 @@ def tile_gatlayer_pa_kernel(tc, q, k, h, w_v, adj, out):
                 scale=-1.0,
                 accum_out=row_sum[i][:, head : head + 1],
             )
-            e_pairs = e[:].bitcast(F32)
+            weights[unit] = e
+
+        def flip_weights(unit):
+            e_pairs = weights[unit][:].bitcast(F32)
             grouped = work.tile([P, NODE_PASSES * P * PACK], BF16, align_bytes=64)
             grouped_pairs = grouped[:].bitcast(F32).rearrange("p (g r u) -> p g r u", r=P, u=2)
             for half in range(2):
@@ -250,19 +280,34 @@ def tile_gatlayer_pa_kernel(tc, q, k, h, w_v, adj, out):
                     )
                 nc.sync.dma_start(out=out[0, cols(i, P), :], in_=result[:])
 
-        load_rows(0)
+        make_penalty(0)
+        flip_keys(0)
         flip_queries(0)
         for c in range(SCORE_BANKS):
             score_matmul(0, c)
+        mask_by_scalar_and_gpsimd(0)
+        flip_keys(1)
         for unit in range(UNITS + 1):
             i, head = divmod(unit, HEADS)
             if head == 0 and i + 1 < ROW_TILES:
                 load_rows(i + 1)
-            if unit >= 1:
-                exponentials_flipped(unit - 1)
             if head == 2 and i + 1 < ROW_TILES:
                 flip_queries(i + 1)
+            if unit + 1 < UNITS:
+                score_matmul(unit + 1, 0)
+            if unit >= 1:
+                exponentials(unit - 1)
+            if unit + 1 < UNITS:
+                mask_by_scalar_and_gpsimd(unit + 1)
+            if head == 1 and i + 1 < ROW_TILES:
+                make_penalty(i + 1)
+            if unit >= 1:
+                flip_weights(unit - 1)
             if unit < UNITS:
-                mask_and_minimum(unit)
+                mask_by_vector_and_minimum(unit)
+            if unit == 0:
+                project_values()
+            if unit + 2 < HEADS:
+                flip_keys(unit + 2)
             if unit >= 1:
                 quantise_and_aggregate(unit - 1)

@@ -146,12 +146,18 @@ def tile_gatlayer_pa_kernel(tc, q, k, h, w_v, adj, out):
 
         k_flipped = keep.tile([P, HEADS, NODES], BF16)
 
+        def copy_flipped(first, out_ap, in_ap):
+            if first:
+                nc.vector.tensor_copy(out=out_ap, in_=in_ap)
+            else:
+                nc.scalar.copy(out=out_ap, in_=in_ap)
+
         def flip_keys(head):
             for c in range(SCORE_BANKS):
                 k_flip = ps_flip.tile([P, BANK], BF16, tag="flip")
                 for t in range(BANK // P):
                     nc.tensor.transpose(k_flip[:, cols(t, P)], k_rows[:, head, (BANK // P) * c + t, :], ident_bf16[:])
-                nc.scalar.copy(out=k_flipped[:, head, cols(c, BANK)], in_=k_flip[:])
+                copy_flipped(head == 0, k_flipped[:, head, cols(c, BANK)], k_flip[:])
 
         q_flipped = {}
         row_sum = {}
@@ -160,12 +166,13 @@ def tile_gatlayer_pa_kernel(tc, q, k, h, w_v, adj, out):
         neg_scores = {}
         neg_max = {}
         weights = {}
+        e_flipped = {}
         e_grouped = {}
 
-        def make_penalty(i):
+        def make_penalty(i, half):
             nc.gpsimd.tensor_scalar(
-                out=penalty[i][:],
-                in0=penalty[i][:],
+                out=penalty[i][:, cols(half, NODES // 2)],
+                in0=penalty[i][:, cols(half, NODES // 2)],
                 scalar1=-HUGE,
                 scalar2=HUGE,
                 op0=ALU.mult,
@@ -173,11 +180,11 @@ def tile_gatlayer_pa_kernel(tc, q, k, h, w_v, adj, out):
             )
 
         def flip_queries(i):
-            q_flip = ps_flip.tile([P, BANK], BF16, tag="flip")
+            q_flip = ps_out.tile([P, BANK], BF16, tag="out")
             for head in range(HEADS):
                 nc.tensor.transpose(q_flip[:, cols(head, P)], q_rows[i][:, head, :], ident_bf16[:])
             q_t = rows.tile([P, HEADS * P], BF16)
-            nc.scalar.copy(out=q_t[:], in_=q_flip[:])
+            copy_flipped(i == 0, q_t[:], q_flip[:])
             q_flipped[i] = q_t
 
         def score_matmul(unit, c):
@@ -192,31 +199,32 @@ def tile_gatlayer_pa_kernel(tc, q, k, h, w_v, adj, out):
             )
             scores[(unit, c)] = s_bank
 
-        def mask_by_scalar_and_gpsimd(unit):
+        def scalar_banks(unit):
+            return 1 + unit % 2
+
+        def mask_by_scalar_and_gpsimd(unit, c):
             i = unit // HEADS
-            x = work.tile([P, NODES], F32)
-            neg_scores[unit] = x
-            nc.scalar.activation(out=x[:, cols(0, BANK)], in_=scores[(unit, 0)][:], func=ACT.Copy, scale=-SCALE)
-            nc.gpsimd.tensor_tensor(
-                out=x[:, cols(0, BANK)], in0=x[:, cols(0, BANK)], in1=penalty[i][:, cols(0, BANK)], op=ALU.add
+            if c == 0:
+                x = work.tile([P, NODES], F32)
+                neg_scores[unit] = x
+            x_bank = neg_scores[unit][:, cols(c, BANK)]
+            nc.scalar.activation(out=x_bank, in_=scores[(unit, c)][:], func=ACT.Copy, scale=-SCALE)
+            nc.gpsimd.tensor_tensor(out=x_bank, in0=x_bank, in1=penalty[i][:, cols(c, BANK)], op=ALU.add)
+
+        def mask_by_vector(unit, c):
+            i = unit // HEADS
+            nc.vector.scalar_tensor_tensor(
+                out=neg_scores[unit][:, cols(c, BANK)],
+                in0=scores[(unit, c)][:],
+                scalar=-SCALE,
+                in1=penalty[i][:, cols(c, BANK)],
+                op0=ALU.mult,
+                op1=ALU.add,
             )
 
-        def mask_by_vector_and_minimum(unit):
-            i = unit // HEADS
-            x = neg_scores[unit]
-            for c in range(1, SCORE_BANKS):
-                nc.vector.scalar_tensor_tensor(
-                    out=x[:, cols(c, BANK)],
-                    in0=scores[(unit, c)][:],
-                    scalar=-SCALE,
-                    in1=penalty[i][:, cols(c, BANK)],
-                    op0=ALU.mult,
-                    op1=ALU.add,
-                )
-                if unit + 1 < UNITS:
-                    score_matmul(unit + 1, c)
+        def row_minimum(unit):
             x_min = work.tile([P, 1], F32)
-            nc.vector.tensor_reduce(out=x_min[:], in_=x[:], axis=AXIS.X, op=ALU.min)
+            nc.vector.tensor_reduce(out=x_min[:], in_=neg_scores[unit][:], axis=AXIS.X, op=ALU.min)
             neg_max[unit] = x_min
 
         def exponentials(unit):
@@ -235,19 +243,24 @@ def tile_gatlayer_pa_kernel(tc, q, k, h, w_v, adj, out):
             )
             weights[unit] = e
 
-        def flip_weights(unit):
+        def flip_weights(unit, half):
             e_pairs = weights[unit][:].bitcast(F32)
-            grouped = work.tile([P, NODE_PASSES * P * PACK], BF16, align_bytes=64)
-            grouped_pairs = grouped[:].bitcast(F32).rearrange("p (g r u) -> p g r u", r=P, u=2)
-            for half in range(2):
-                e_flip = ps_flip.tile([P, BANK], F32, tag="flip")
-                for t in range(4):
-                    nc.tensor.transpose(e_flip[:, cols(t, P)], e_pairs[:, cols(4 * half + t, P)], ident_f32[:])
-                nc.scalar.copy(
-                    out=grouped_pairs[:, cols(half, 2), :, :],
-                    in_=e_flip[:].rearrange("p (g u r) -> p g r u", g=2, u=2),
+            e_flip = ps_flip.tile([P, BANK], F32, tag="flip")
+            for t in range(BANK // P):
+                nc.tensor.transpose(
+                    e_flip[:, cols(t, P)], e_pairs[:, cols((BANK // P) * half + t, P)], ident_f32[:]
                 )
-            e_grouped[unit] = grouped
+            e_flipped[(unit, half)] = e_flip
+
+        def group_weights(unit, half):
+            if half == 0:
+                grouped = work.tile([P, NODE_PASSES * P * PACK], BF16, align_bytes=64)
+                e_grouped[unit] = grouped
+            grouped_pairs = e_grouped[unit][:].bitcast(F32).rearrange("p (g r u) -> p g r u", r=P, u=2)
+            nc.scalar.copy(
+                out=grouped_pairs[:, cols(half, 2), :, :],
+                in_=e_flipped[(unit, half)][:].rearrange("p (g u r) -> p g r u", g=2, u=2),
+            )
 
         def quantise_and_aggregate(unit):
             i, head = divmod(unit, HEADS)
@@ -267,47 +280,62 @@ def tile_gatlayer_pa_kernel(tc, q, k, h, w_v, adj, out):
                     start=(g == 0),
                     stop=(g == NODE_PASSES - 1),
                 )
-            if head == HEADS - 1:
-                inverse = rows.tile([P, HEADS], F32)
-                nc.vector.reciprocal(out=inverse[:], in_=row_sum[i][:])
-                result = rows.tile([P, FEATURES], F32)
-                for n in range(HEADS):
-                    nc.scalar.activation(
-                        out=result[:, cols(n, HEAD_DIM)],
-                        in_=out_sum[i][:, cols(n, HEAD_DIM)],
-                        func=ACT.Copy,
-                        scale=inverse[:, n : n + 1],
-                    )
-                nc.sync.dma_start(out=out[0, cols(i, P), :], in_=result[:])
 
-        make_penalty(0)
+        def finish_rows(i):
+            inverse = rows.tile([P, HEADS], F32)
+            nc.vector.reciprocal(out=inverse[:], in_=row_sum[i][:])
+            result = rows.tile([P, FEATURES], F32)
+            for head in range(HEADS):
+                nc.scalar.activation(
+                    out=result[:, cols(head, HEAD_DIM)],
+                    in_=out_sum[i][:, cols(head, HEAD_DIM)],
+                    func=ACT.Copy,
+                    scale=inverse[:, head : head + 1],
+                )
+            nc.sync.dma_start(out=out[0, cols(i, P), :], in_=result[:])
+
+        def step(n):
+            i, head = divmod(n, HEADS)
+            more_rows = i + 1 < ROW_TILES
+            if head == 0 and more_rows:
+                load_rows(i + 1)
+            if head in (1, 2) and more_rows:
+                make_penalty(i + 1, head - 1)
+            if 0 <= n - 1 < UNITS:
+                exponentials(n - 1)
+            for c in range(SCORE_BANKS):
+                if n < UNITS and c >= scalar_banks(n):
+                    mask_by_vector(n, c)
+                if n + 1 < UNITS:
+                    score_matmul(n + 1, c)
+                    if c < scalar_banks(n + 1):
+                        mask_by_scalar_and_gpsimd(n + 1, c)
+            if n < UNITS:
+                row_minimum(n)
+            for half in range(2):
+                if 0 <= n - 2 < UNITS:
+                    group_weights(n - 2, half)
+                if 0 <= n - 1 < UNITS:
+                    flip_weights(n - 1, half)
+            if head == 1 and more_rows:
+                flip_queries(i + 1)
+            if head == 3 and i >= 1:
+                finish_rows(i - 1)
+            if n == 0:
+                project_values()
+            if n + 2 < HEADS:
+                flip_keys(n + 2)
+            if 0 <= n - 3:
+                quantise_and_aggregate(n - 3)
+
+        make_penalty(0, 0)
+        make_penalty(0, 1)
         flip_keys(0)
         flip_queries(0)
         for c in range(SCORE_BANKS):
             score_matmul(0, c)
-        mask_by_scalar_and_gpsimd(0)
+        mask_by_scalar_and_gpsimd(0, 0)
         flip_keys(1)
-        for unit in range(UNITS + 1):
-            i, head = divmod(unit, HEADS)
-            if head == 0 and i + 1 < ROW_TILES:
-                load_rows(i + 1)
-            if head == 2 and i + 1 < ROW_TILES:
-                flip_queries(i + 1)
-            if unit + 1 < UNITS:
-                score_matmul(unit + 1, 0)
-            if unit >= 1:
-                exponentials(unit - 1)
-            if unit + 1 < UNITS:
-                mask_by_scalar_and_gpsimd(unit + 1)
-            if head == 1 and i + 1 < ROW_TILES:
-                make_penalty(i + 1)
-            if unit >= 1:
-                flip_weights(unit - 1)
-            if unit < UNITS:
-                mask_by_vector_and_minimum(unit)
-            if unit == 0:
-                project_values()
-            if unit + 2 < HEADS:
-                flip_keys(unit + 2)
-            if unit >= 1:
-                quantise_and_aggregate(unit - 1)
+        for n in range(UNITS + 3):
+            step(n)
+        finish_rows(ROW_TILES - 1)

@@ -27,6 +27,7 @@ ROW_TILES = NODES // P
 UNITS = ROW_TILES * HEADS
 SCORE_BANKS = NODES // BANK
 NODE_PASSES = NODES // K_PASS
+SCALAR_BANKS = 1
 SCALE = 1.0 / math.sqrt(HEAD_DIM)
 HUGE = 3.0e38
 
@@ -159,7 +160,9 @@ def tile_gatlayer_pa_kernel(tc, q, k, h, w_v, adj, out):
                     nc.tensor.transpose(k_flip[:, cols(t, P)], k_rows[:, head, (BANK // P) * c + t, :], ident_bf16[:])
                 copy_flipped(head == 0, k_flipped[:, head, cols(c, BANK)], k_flip[:])
 
+        q_in_psum = {}
         q_flipped = {}
+        inverse_sum = {}
         row_sum = {}
         out_sum = {}
         scores = {}
@@ -183,8 +186,11 @@ def tile_gatlayer_pa_kernel(tc, q, k, h, w_v, adj, out):
             q_flip = ps_out.tile([P, BANK], BF16, tag="out")
             for head in range(HEADS):
                 nc.tensor.transpose(q_flip[:, cols(head, P)], q_rows[i][:, head, :], ident_bf16[:])
+            q_in_psum[i] = q_flip
+
+        def keep_queries(i):
             q_t = rows.tile([P, HEADS * P], BF16)
-            copy_flipped(i == 0, q_t[:], q_flip[:])
+            copy_flipped(i == 0, q_t[:], q_in_psum[i][:])
             q_flipped[i] = q_t
 
         def score_matmul(unit, c):
@@ -198,9 +204,6 @@ def tile_gatlayer_pa_kernel(tc, q, k, h, w_v, adj, out):
                 stop=True,
             )
             scores[(unit, c)] = s_bank
-
-        def scalar_banks(unit):
-            return 1 + unit % 2
 
         def mask_by_scalar_and_gpsimd(unit, c):
             i = unit // HEADS
@@ -281,9 +284,13 @@ def tile_gatlayer_pa_kernel(tc, q, k, h, w_v, adj, out):
                     stop=(g == NODE_PASSES - 1),
                 )
 
-        def finish_rows(i):
+        def invert_row_sums(i):
             inverse = rows.tile([P, HEADS], F32)
             nc.vector.reciprocal(out=inverse[:], in_=row_sum[i][:])
+            inverse_sum[i] = inverse
+
+        def finish_rows(i):
+            inverse = inverse_sum[i]
             result = rows.tile([P, FEATURES], F32)
             for head in range(HEADS):
                 nc.scalar.activation(
@@ -301,15 +308,25 @@ def tile_gatlayer_pa_kernel(tc, q, k, h, w_v, adj, out):
                 load_rows(i + 1)
             if head in (1, 2) and more_rows:
                 make_penalty(i + 1, head - 1)
+            if head == 1 and more_rows:
+                flip_queries(i + 1)
+            if head == 3 and i >= 1:
+                invert_row_sums(i - 1)
             if 0 <= n - 1 < UNITS:
                 exponentials(n - 1)
             for c in range(SCORE_BANKS):
-                if n < UNITS and c >= scalar_banks(n):
+                if n < UNITS and c >= SCALAR_BANKS:
                     mask_by_vector(n, c)
                 if n + 1 < UNITS:
                     score_matmul(n + 1, c)
-                    if c < scalar_banks(n + 1):
+                    if c < SCALAR_BANKS:
                         mask_by_scalar_and_gpsimd(n + 1, c)
+            if n == 0:
+                project_values()
+            if head == 3 and i >= 1:
+                finish_rows(i - 1)
+            if 0 <= n - 3:
+                quantise_and_aggregate(n - 3)
             if n < UNITS:
                 row_minimum(n)
             for half in range(2):
@@ -318,24 +335,23 @@ def tile_gatlayer_pa_kernel(tc, q, k, h, w_v, adj, out):
                 if 0 <= n - 1 < UNITS:
                     flip_weights(n - 1, half)
             if head == 1 and more_rows:
-                flip_queries(i + 1)
-            if head == 3 and i >= 1:
-                finish_rows(i - 1)
-            if n == 0:
-                project_values()
+                keep_queries(i + 1)
             if n + 2 < HEADS:
                 flip_keys(n + 2)
-            if 0 <= n - 3:
-                quantise_and_aggregate(n - 3)
 
         make_penalty(0, 0)
         make_penalty(0, 1)
         flip_keys(0)
         flip_queries(0)
+        keep_queries(0)
         for c in range(SCORE_BANKS):
             score_matmul(0, c)
         mask_by_scalar_and_gpsimd(0, 0)
         flip_keys(1)
-        for n in range(UNITS + 3):
+        for n in range(HEADS):
             step(n)
-        finish_rows(ROW_TILES - 1)
+        with tc.manual_schedule():
+            for n in range(HEADS, UNITS + 3):
+                step(n)
+            invert_row_sums(ROW_TILES - 1)
+            finish_rows(ROW_TILES - 1)

@@ -27,7 +27,6 @@ ROW_TILES = NODES // P
 UNITS = ROW_TILES * HEADS
 SCORE_BANKS = NODES // BANK
 NODE_PASSES = NODES // K_PASS
-SCALAR_BANKS = 1
 SCALE = 1.0 / math.sqrt(HEAD_DIM)
 HUGE = 3.0e38
 
@@ -103,6 +102,12 @@ def tile_gatlayer_pa_kernel(tc, q, k, h, w_v, adj, out):
         v_codes = keep.tile([P, NODE_PASSES, FEATURES], U32, align_bytes=64)
         v_scales = keep.tile([P, NODE_PASSES, FEATURES], U8, align_bytes=64)
 
+        def shared_copy(piece, out_ap, in_ap):
+            if piece % 2 == 0:
+                nc.vector.tensor_copy(out=out_ap, in_=in_ap)
+            else:
+                nc.scalar.copy(out=out_ap, in_=in_ap)
+
         def project_values():
             w_grouped = stage.tile([P, FEATURES * PACK], BF16, align_bytes=64)
             regroup(w_grouped, w_rows)
@@ -115,9 +120,10 @@ def tile_gatlayer_pa_kernel(tc, q, k, h, w_v, adj, out):
                     for u in range(2):
                         nc.tensor.transpose(h_flip[:, cols(2 * b + u, P)], h_pairs[:, cols(u, P)], ident_f32[:])
                 h_grouped = stage.tile([P, 2 * P * PACK], BF16, align_bytes=64)
-                nc.scalar.copy(
-                    out=h_grouped[:].bitcast(F32).rearrange("p (b r u) -> p b r u", b=2, u=2),
-                    in_=h_flip[:].rearrange("p (b u r) -> p b r u", b=2, u=2),
+                shared_copy(
+                    a,
+                    h_grouped[:].bitcast(F32).rearrange("p (b r u) -> p b r u", b=2, u=2),
+                    h_flip[:].rearrange("p (b u r) -> p b r u", b=2, u=2),
                 )
                 nc.vector.quantize_mx(
                     out=h_codes[:, cols(a, 2 * P)].bitcast(FP8X4),
@@ -138,7 +144,7 @@ def tile_gatlayer_pa_kernel(tc, q, k, h, w_v, adj, out):
                         start=True,
                         stop=True,
                     )
-                    nc.scalar.copy(out=v_rows[:, t, :], in_=v_sum[:])
+                    shared_copy(t, v_rows[:, t, :], v_sum[:])
                 v_grouped = stage.tile([P, FEATURES * PACK], BF16, align_bytes=64)
                 regroup(v_grouped, v_rows)
                 nc.vector.quantize_mx(
@@ -204,6 +210,9 @@ def tile_gatlayer_pa_kernel(tc, q, k, h, w_v, adj, out):
                 stop=True,
             )
             scores[(unit, c)] = s_bank
+
+        def scalar_banks(unit):
+            return 2 if unit % HEADS == 0 else 1
 
         def mask_by_scalar_and_gpsimd(unit, c):
             i = unit // HEADS
@@ -315,11 +324,11 @@ def tile_gatlayer_pa_kernel(tc, q, k, h, w_v, adj, out):
             if 0 <= n - 1 < UNITS:
                 exponentials(n - 1)
             for c in range(SCORE_BANKS):
-                if n < UNITS and c >= SCALAR_BANKS:
+                if n < UNITS and c >= scalar_banks(n):
                     mask_by_vector(n, c)
                 if n + 1 < UNITS:
                     score_matmul(n + 1, c)
-                    if c < SCALAR_BANKS:
+                    if c < scalar_banks(n + 1):
                         mask_by_scalar_and_gpsimd(n + 1, c)
             if n == 0:
                 project_values()
@@ -346,7 +355,8 @@ def tile_gatlayer_pa_kernel(tc, q, k, h, w_v, adj, out):
         keep_queries(0)
         for c in range(SCORE_BANKS):
             score_matmul(0, c)
-        mask_by_scalar_and_gpsimd(0, 0)
+        for c in range(scalar_banks(0)):
+            mask_by_scalar_and_gpsimd(0, c)
         flip_keys(1)
         for n in range(HEADS):
             step(n)

@@ -27,6 +27,7 @@ ROW_TILES = NODES // P
 UNITS = ROW_TILES * HEADS
 SCORE_BANKS = NODES // BANK
 NODE_PASSES = NODES // K_PASS
+SCALAR_BANKS = 1
 SCALE = 1.0 / math.sqrt(HEAD_DIM)
 HUGE = 3.0e38
 
@@ -211,9 +212,6 @@ def tile_gatlayer_pa_kernel(tc, q, k, h, w_v, adj, out):
             )
             scores[(unit, c)] = s_bank
 
-        def scalar_banks(unit):
-            return 2 if unit % HEADS == 0 else 1
-
         def mask_by_scalar_and_gpsimd(unit, c):
             i = unit // HEADS
             if c == 0:
@@ -324,11 +322,11 @@ def tile_gatlayer_pa_kernel(tc, q, k, h, w_v, adj, out):
             if 0 <= n - 1 < UNITS:
                 exponentials(n - 1)
             for c in range(SCORE_BANKS):
-                if n < UNITS and c >= scalar_banks(n):
+                if n < UNITS and c >= SCALAR_BANKS:
                     mask_by_vector(n, c)
                 if n + 1 < UNITS:
                     score_matmul(n + 1, c)
-                    if c < scalar_banks(n + 1):
+                    if c < SCALAR_BANKS:
                         mask_by_scalar_and_gpsimd(n + 1, c)
             if n == 0:
                 project_values()
@@ -355,8 +353,7 @@ def tile_gatlayer_pa_kernel(tc, q, k, h, w_v, adj, out):
         keep_queries(0)
         for c in range(SCORE_BANKS):
             score_matmul(0, c)
-        for c in range(scalar_banks(0)):
-            mask_by_scalar_and_gpsimd(0, c)
+        mask_by_scalar_and_gpsimd(0, 0)
         flip_keys(1)
         for n in range(HEADS):
             step(n)

@@ -27,7 +27,9 @@ ROW_TILES = NODES // P
 UNITS = ROW_TILES * HEADS
 SCORE_BANKS = NODES // BANK
 NODE_PASSES = NODES // K_PASS
-SCALAR_BANKS = 1
+TENSOR_BANKS = 3
+BANK_ORDER = (3, 0, 1, 2)
+CHUNKS = 2 * TENSOR_BANKS
 SCALE = 1.0 / math.sqrt(HEAD_DIM)
 HUGE = 3.0e38
 
@@ -46,7 +48,8 @@ def tile_gatlayer_pa_kernel(tc, q, k, h, w_v, adj, out):
         work = ctx.enter_context(tc.tile_pool(name="work", bufs=3))
         ps_prod = ctx.enter_context(tc.psum_pool(name="ps_prod", bufs=4))
         ps_flip = ctx.enter_context(tc.psum_pool(name="ps_flip", bufs=2))
-        ps_out = ctx.enter_context(tc.psum_pool(name="ps_out", bufs=2))
+        ps_out = ctx.enter_context(tc.psum_pool(name="ps_out", bufs=1))
+        ps_misc = ctx.enter_context(tc.psum_pool(name="ps_misc", bufs=1))
 
         ident_f32 = const.tile([P, P], F32)
         make_identity(nc, ident_f32[:])
@@ -64,34 +67,36 @@ def tile_gatlayer_pa_kernel(tc, q, k, h, w_v, adj, out):
             )
 
         q_rows = {}
-        penalty = {}
+        adj_rows = {}
 
         def load_rows(i):
             q_tile = rows.tile([P, HEADS, HEAD_DIM], BF16)
             nc.sync.dma_start(out=q_tile[:], in_=q[0, :, cols(i, P), :].rearrange("n p d -> p n d"))
             q_rows[i] = q_tile
-            pen = rows.tile([P, NODES], BF16)
-            nc.sync.dma_start(out=pen[:], in_=adj[cols(i, P), :])
-            penalty[i] = pen
+            adj_tile = rows.tile([P, NODES], BF16)
+            nc.sync.dma_start(out=adj_tile[:], in_=adj[cols(i, P), :])
+            adj_rows[i] = adj_tile
 
-        k_rows = keep.tile([P, HEADS, ROW_TILES, HEAD_DIM], BF16)
+        k_rows = keep.tile([P, HEADS, ROW_TILES // 2, 2, HEAD_DIM], BF16)
 
         def load_keys(head):
-            nc.sync.dma_start(out=k_rows[:, head, :, :], in_=k[0, head].rearrange("(t p) d -> p t d", p=P))
+            nc.sync.dma_start(
+                out=k_rows[:, head, :, :, :], in_=k[0, head].rearrange("(m p b) d -> p m b d", p=P, b=2)
+            )
 
         load_keys(0)
         load_rows(0)
         load_keys(1)
+        load_rows(1)
         w_rows = keep.tile([P, PACK, FEATURES], BF16)
         nc.sync.dma_start(
             out=w_rows[:].rearrange("p (u b) c -> p u b c", u=2),
             in_=w_v.rearrange("(u p b) c -> p u b c", u=2, b=2),
         )
-        h_rows = keep.tile([P, NODES // (2 * P), 2, FEATURES], BF16)
+        h_rows = keep.tile([P, NODE_PASSES, PACK, FEATURES], BF16)
         for g in range(NODE_PASSES):
             nc.sync.dma_start(
-                out=h_rows[:, cols(g, 2), :, :],
-                in_=h[0, cols(g, K_PASS), :].rearrange("(a p b) k -> p a b k", a=2, b=2),
+                out=h_rows[:, g, :, :], in_=h[0, cols(g, K_PASS), :].rearrange("(p s) k -> p s k", s=PACK)
             )
         load_keys(2)
         load_keys(3)
@@ -117,7 +122,7 @@ def tile_gatlayer_pa_kernel(tc, q, k, h, w_v, adj, out):
             for a in range(NODES // (2 * P)):
                 h_flip = ps_flip.tile([P, BANK], F32, tag="flip")
                 for b in range(2):
-                    h_pairs = h_rows[:, a, b, :].bitcast(F32)
+                    h_pairs = h_rows[:, a // 2, 2 * b + a % 2, :].bitcast(F32)
                     for u in range(2):
                         nc.tensor.transpose(h_flip[:, cols(2 * b + u, P)], h_pairs[:, cols(u, P)], ident_f32[:])
                 h_grouped = stage.tile([P, 2 * P * PACK], BF16, align_bytes=64)
@@ -135,7 +140,10 @@ def tile_gatlayer_pa_kernel(tc, q, k, h, w_v, adj, out):
             for g in range(NODE_PASSES):
                 v_rows = stage.tile([P, PACK, FEATURES], BF16)
                 for t in range(PACK):
-                    v_sum = ps_out.tile([P, BANK], F32, tag="out")
+                    if t % 2 == 0:
+                        v_sum = ps_out.tile([P, BANK], F32, tag="out")
+                    else:
+                        v_sum = ps_misc.tile([P, BANK], F32, tag="misc")
                     nc.tensor.matmul_mx(
                         out=v_sum[:],
                         lhsT=h_codes[:, cols(PACK * g + t, P)].bitcast(FP8X4),
@@ -164,9 +172,15 @@ def tile_gatlayer_pa_kernel(tc, q, k, h, w_v, adj, out):
             for c in range(SCORE_BANKS):
                 k_flip = ps_flip.tile([P, BANK], BF16, tag="flip")
                 for t in range(BANK // P):
-                    nc.tensor.transpose(k_flip[:, cols(t, P)], k_rows[:, head, (BANK // P) * c + t, :], ident_bf16[:])
+                    b, m = divmod(t, 2)
+                    nc.tensor.transpose(k_flip[:, cols(t, P)], k_rows[:, head, 2 * c + m, b, :], ident_bf16[:])
                 copy_flipped(head == 0, k_flipped[:, head, cols(c, BANK)], k_flip[:])
 
+        edges_in_psum = {}
+        edges_flipped = {}
+        penalty_t = {}
+        penalty_v = {}
+        minima = {}
         q_in_psum = {}
         q_flipped = {}
         inverse_sum = {}
@@ -178,19 +192,53 @@ def tile_gatlayer_pa_kernel(tc, q, k, h, w_v, adj, out):
         weights = {}
         e_flipped = {}
         e_grouped = {}
+        e_quantised = {}
 
-        def make_penalty(i, half):
+        def flip_edges(i, first):
+            words = adj_rows[i][:].bitcast(F32)
+            bank = ps_misc.tile([P, BANK], F32, tag="misc")
+            for c in range(first, min(first + 4, CHUNKS)):
+                nc.tensor.transpose(bank[:, cols(c - first, P)], words[:, cols(c, P)], ident_f32[:])
+            edges_in_psum[(i, first)] = bank
+
+        def keep_edges(i, first):
+            if first == 0:
+                flipped = rows.tile([P, CHUNKS * P], F32)
+                edges_flipped[i] = flipped
+            last = min(first + 4, CHUNKS)
+            nc.scalar.copy(
+                out=edges_flipped[i][:, first * P : last * P],
+                in_=edges_in_psum[(i, first)][:, : (last - first) * P],
+            )
+
+        def penalty_for_tensor(i, g):
+            if g == 0:
+                pen = rows.tile([P, TENSOR_BANKS, 2, 2, P], F32)
+                penalty_t[i] = pen
+            edges = edges_flipped[i][:].bitcast(BF16)[:, cols(g, 4 * P)]
             nc.gpsimd.tensor_scalar(
-                out=penalty[i][:, cols(half, NODES // 2)],
-                in0=penalty[i][:, cols(half, NODES // 2)],
+                out=penalty_t[i][:, g, :, :, :],
+                in0=edges.rearrange("p (m i b) -> p m b i", m=2, b=2),
+                scalar1=HUGE,
+                scalar2=-HUGE,
+                op0=ALU.mult,
+                op1=ALU.add,
+            )
+
+        def penalty_for_vector(i):
+            pen = rows.tile([P, BANK], BF16)
+            nc.gpsimd.tensor_scalar(
+                out=pen[:].rearrange("p (b y) -> p b y", b=2),
+                in0=adj_rows[i][:, cols(TENSOR_BANKS, BANK)].rearrange("p (y b) -> p b y", b=2),
                 scalar1=-HUGE,
                 scalar2=HUGE,
                 op0=ALU.mult,
                 op1=ALU.add,
             )
+            penalty_v[i] = pen
 
         def flip_queries(i):
-            q_flip = ps_out.tile([P, BANK], BF16, tag="out")
+            q_flip = ps_misc.tile([P, BANK], BF16, tag="misc")
             for head in range(HEADS):
                 nc.tensor.transpose(q_flip[:, cols(head, P)], q_rows[i][:, head, :], ident_bf16[:])
             q_in_psum[i] = q_flip
@@ -203,23 +251,37 @@ def tile_gatlayer_pa_kernel(tc, q, k, h, w_v, adj, out):
         def score_matmul(unit, c):
             i, head = divmod(unit, HEADS)
             s_bank = ps_prod.tile([P, BANK], F32, tag="prod")
+            masked = c < TENSOR_BANKS
             nc.tensor.matmul(
                 out=s_bank[:],
                 lhsT=q_flipped[i][:, cols(head, P)],
                 rhs=k_flipped[:, head, cols(c, BANK)],
                 start=True,
-                stop=True,
+                stop=not masked,
             )
+            if masked:
+                for t in range(BANK // P):
+                    b, m = divmod(t, 2)
+                    nc.tensor.matmul(
+                        out=s_bank[:, cols(t, P)],
+                        lhsT=penalty_t[i][:, c, m, b, :],
+                        rhs=ident_f32[:],
+                        start=False,
+                        stop=(t == BANK // P - 1),
+                        is_transpose=True,
+                    )
             scores[(unit, c)] = s_bank
 
-        def mask_by_scalar_and_gpsimd(unit, c):
-            i = unit // HEADS
-            if c == 0:
-                x = work.tile([P, NODES], F32)
-                neg_scores[unit] = x
-            x_bank = neg_scores[unit][:, cols(c, BANK)]
-            nc.scalar.activation(out=x_bank, in_=scores[(unit, c)][:], func=ACT.Copy, scale=-SCALE)
-            nc.gpsimd.tensor_tensor(out=x_bank, in0=x_bank, in1=penalty[i][:, cols(c, BANK)], op=ALU.add)
+        def scale_masked(unit, c):
+            nc.vector.tensor_scalar(
+                out=neg_scores[unit][:, cols(c, BANK)],
+                in0=scores[(unit, c)][:],
+                scalar1=-SCALE,
+                scalar2=None,
+                op0=ALU.mult,
+                op1=ALU.min,
+                accum_out=minima[unit][:, c : c + 1],
+            )
 
         def mask_by_vector(unit, c):
             i = unit // HEADS
@@ -227,14 +289,30 @@ def tile_gatlayer_pa_kernel(tc, q, k, h, w_v, adj, out):
                 out=neg_scores[unit][:, cols(c, BANK)],
                 in0=scores[(unit, c)][:],
                 scalar=-SCALE,
-                in1=penalty[i][:, cols(c, BANK)],
+                in1=penalty_v[i][:],
                 op0=ALU.mult,
                 op1=ALU.add,
             )
 
+        def empty_bank(unit, c):
+            if c == BANK_ORDER[0]:
+                x = work.tile([P, NODES], F32)
+                neg_scores[unit] = x
+                mins = work.tile([P, SCORE_BANKS], F32)
+                minima[unit] = mins
+            if c < TENSOR_BANKS:
+                scale_masked(unit, c)
+            else:
+                mask_by_vector(unit, c)
+
+        def bank_minimum(unit, c):
+            nc.vector.tensor_reduce(
+                out=minima[unit][:, c : c + 1], in_=neg_scores[unit][:, cols(c, BANK)], axis=AXIS.X, op=ALU.min
+            )
+
         def row_minimum(unit):
             x_min = work.tile([P, 1], F32)
-            nc.vector.tensor_reduce(out=x_min[:], in_=neg_scores[unit][:], axis=AXIS.X, op=ALU.min)
+            nc.vector.tensor_reduce(out=x_min[:], in_=minima[unit][:], axis=AXIS.X, op=ALU.min)
             neg_max[unit] = x_min
 
         def exponentials(unit):
@@ -272,11 +350,15 @@ def tile_gatlayer_pa_kernel(tc, q, k, h, w_v, adj, out):
                 in_=e_flipped[(unit, half)][:].rearrange("p (g u r) -> p g r u", g=2, u=2),
             )
 
-        def quantise_and_aggregate(unit):
-            i, head = divmod(unit, HEADS)
+        def quantise(unit):
             e_codes = work.tile([P, NODE_PASSES * P], U32, align_bytes=64)
             e_scales = work.tile([P, NODE_PASSES * P], U8, align_bytes=64)
             nc.vector.quantize_mx(out=e_codes[:].bitcast(FP8X4), scales=e_scales[:], in_=e_grouped[unit][:])
+            e_quantised[unit] = (e_codes, e_scales)
+
+        def aggregate(unit):
+            i, head = divmod(unit, HEADS)
+            e_codes, e_scales = e_quantised[unit]
             if head == 0:
                 o_bank = ps_out.tile([P, BANK], F32, tag="out")
                 out_sum[i] = o_bank
@@ -310,55 +392,70 @@ def tile_gatlayer_pa_kernel(tc, q, k, h, w_v, adj, out):
 
         def step(n):
             i, head = divmod(n, HEADS)
-            more_rows = i + 1 < ROW_TILES
-            if head == 0 and more_rows:
-                load_rows(i + 1)
-            if head in (1, 2) and more_rows:
-                make_penalty(i + 1, head - 1)
-            if head == 1 and more_rows:
-                flip_queries(i + 1)
-            if head == 3 and i >= 1:
+            if head == 0 and i + 2 < ROW_TILES:
+                load_rows(i + 2)
+            if head == 2 and i >= 1 and i - 1 < ROW_TILES:
                 invert_row_sums(i - 1)
+            if head == 0 and i >= 2:
+                finish_rows(i - 2)
             if 0 <= n - 1 < UNITS:
                 exponentials(n - 1)
-            for c in range(SCORE_BANKS):
-                if n < UNITS and c >= SCALAR_BANKS:
-                    mask_by_vector(n, c)
+            for place, c in enumerate(BANK_ORDER):
+                if n < UNITS:
+                    empty_bank(n, c)
                 if n + 1 < UNITS:
                     score_matmul(n + 1, c)
-                    if c < SCALAR_BANKS:
-                        mask_by_scalar_and_gpsimd(n + 1, c)
+                if place < 2 and 0 <= n - 2 < UNITS:
+                    flip_weights(n - 2, place)
+                if place == 2 and 0 <= n - 4 < UNITS:
+                    aggregate(n - 4)
             if n == 0:
                 project_values()
-            if head == 3 and i >= 1:
-                finish_rows(i - 1)
-            if 0 <= n - 3:
-                quantise_and_aggregate(n - 3)
+            if n < UNITS:
+                bank_minimum(n, TENSOR_BANKS)
+            if 0 <= n - 3 < UNITS:
+                quantise(n - 3)
             if n < UNITS:
                 row_minimum(n)
+            if head == 0 and i + 1 < ROW_TILES:
+                if i >= 1:
+                    keep_queries(i + 1)
+                flip_edges(i + 1, 0)
+            if head == 1 and i + 1 < ROW_TILES:
+                keep_edges(i + 1, 0)
+                flip_edges(i + 1, 4)
+                penalty_for_tensor(i + 1, 0)
+                penalty_for_tensor(i + 1, 1)
+            if head == 2 and i + 1 < ROW_TILES:
+                keep_edges(i + 1, 4)
+                penalty_for_tensor(i + 1, 2)
+                penalty_for_vector(i + 1)
+            if head == 3 and i + 2 < ROW_TILES:
+                flip_queries(i + 2)
             for half in range(2):
                 if 0 <= n - 2 < UNITS:
                     group_weights(n - 2, half)
-                if 0 <= n - 1 < UNITS:
-                    flip_weights(n - 1, half)
-            if head == 1 and more_rows:
-                keep_queries(i + 1)
             if n + 2 < HEADS:
                 flip_keys(n + 2)
 
-        make_penalty(0, 0)
-        make_penalty(0, 1)
         flip_keys(0)
         flip_queries(0)
         keep_queries(0)
-        for c in range(SCORE_BANKS):
+        flip_edges(0, 0)
+        keep_edges(0, 0)
+        flip_edges(0, 4)
+        keep_edges(0, 4)
+        for g in range(TENSOR_BANKS):
+            penalty_for_tensor(0, g)
+        penalty_for_vector(0)
+        for c in BANK_ORDER:
             score_matmul(0, c)
-        mask_by_scalar_and_gpsimd(0, 0)
         flip_keys(1)
+        flip_queries(1)
+        keep_queries(1)
         for n in range(HEADS):
             step(n)
         with tc.manual_schedule():
-            for n in range(HEADS, UNITS + 3):
+            for n in range(HEADS, UNITS + 4):
                 step(n)
-            invert_row_sums(ROW_TILES - 1)
             finish_rows(ROW_TILES - 1)

@@ -27,9 +27,7 @@ ROW_TILES = NODES // P
 UNITS = ROW_TILES * HEADS
 SCORE_BANKS = NODES // BANK
 NODE_PASSES = NODES // K_PASS
-TENSOR_BANKS = 3
-BANK_ORDER = (3, 0, 1, 2)
-CHUNKS = 2 * TENSOR_BANKS
+CHUNKS = NODES // (2 * P)
 SCALE = 1.0 / math.sqrt(HEAD_DIM)
 HUGE = 3.0e38
 
@@ -179,7 +177,6 @@ def tile_gatlayer_pa_kernel(tc, q, k, h, w_v, adj, out):
         edges_in_psum = {}
         edges_flipped = {}
         penalty_t = {}
-        penalty_v = {}
         minima = {}
         q_in_psum = {}
         q_flipped = {}
@@ -197,7 +194,7 @@ def tile_gatlayer_pa_kernel(tc, q, k, h, w_v, adj, out):
         def flip_edges(i, first):
             words = adj_rows[i][:].bitcast(F32)
             bank = ps_misc.tile([P, BANK], F32, tag="misc")
-            for c in range(first, min(first + 4, CHUNKS)):
+            for c in range(first, first + 4):
                 nc.tensor.transpose(bank[:, cols(c - first, P)], words[:, cols(c, P)], ident_f32[:])
             edges_in_psum[(i, first)] = bank
 
@@ -205,15 +202,11 @@ def tile_gatlayer_pa_kernel(tc, q, k, h, w_v, adj, out):
             if first == 0:
                 flipped = rows.tile([P, CHUNKS * P], F32)
                 edges_flipped[i] = flipped
-            last = min(first + 4, CHUNKS)
-            nc.scalar.copy(
-                out=edges_flipped[i][:, first * P : last * P],
-                in_=edges_in_psum[(i, first)][:, : (last - first) * P],
-            )
+            nc.vector.tensor_copy(out=edges_flipped[i][:, cols(first // 4, BANK)], in_=edges_in_psum[(i, first)][:])
 
         def penalty_for_tensor(i, g):
             if g == 0:
-                pen = rows.tile([P, TENSOR_BANKS, 2, 2, P], F32)
+                pen = rows.tile([P, SCORE_BANKS, 2, 2, P], F32)
                 penalty_t[i] = pen
             edges = edges_flipped[i][:].bitcast(BF16)[:, cols(g, 4 * P)]
             nc.gpsimd.tensor_scalar(
@@ -224,18 +217,6 @@ def tile_gatlayer_pa_kernel(tc, q, k, h, w_v, adj, out):
                 op0=ALU.mult,
                 op1=ALU.add,
             )
-
-        def penalty_for_vector(i):
-            pen = rows.tile([P, BANK], BF16)
-            nc.gpsimd.tensor_scalar(
-                out=pen[:].rearrange("p (b y) -> p b y", b=2),
-                in0=adj_rows[i][:, cols(TENSOR_BANKS, BANK)].rearrange("p (y b) -> p b y", b=2),
-                scalar1=-HUGE,
-                scalar2=HUGE,
-                op0=ALU.mult,
-                op1=ALU.add,
-            )
-            penalty_v[i] = pen
 
         def flip_queries(i):
             q_flip = ps_misc.tile([P, BANK], BF16, tag="misc")
@@ -251,28 +232,31 @@ def tile_gatlayer_pa_kernel(tc, q, k, h, w_v, adj, out):
         def score_matmul(unit, c):
             i, head = divmod(unit, HEADS)
             s_bank = ps_prod.tile([P, BANK], F32, tag="prod")
-            masked = c < TENSOR_BANKS
             nc.tensor.matmul(
                 out=s_bank[:],
                 lhsT=q_flipped[i][:, cols(head, P)],
                 rhs=k_flipped[:, head, cols(c, BANK)],
                 start=True,
-                stop=not masked,
+                stop=False,
             )
-            if masked:
-                for t in range(BANK // P):
-                    b, m = divmod(t, 2)
-                    nc.tensor.matmul(
-                        out=s_bank[:, cols(t, P)],
-                        lhsT=penalty_t[i][:, c, m, b, :],
-                        rhs=ident_f32[:],
-                        start=False,
-                        stop=(t == BANK // P - 1),
-                        is_transpose=True,
-                    )
+            for t in range(BANK // P):
+                b, m = divmod(t, 2)
+                nc.tensor.matmul(
+                    out=s_bank[:, cols(t, P)],
+                    lhsT=penalty_t[i][:, c, m, b, :],
+                    rhs=ident_f32[:],
+                    start=False,
+                    stop=(t == BANK // P - 1),
+                    is_transpose=True,
+                )
             scores[(unit, c)] = s_bank
 
-        def scale_masked(unit, c):
+        def empty_bank(unit, c):
+            if c == 0:
+                x = work.tile([P, NODES], F32)
+                neg_scores[unit] = x
+                mins = work.tile([P, SCORE_BANKS], F32)
+                minima[unit] = mins
             nc.vector.tensor_scalar(
                 out=neg_scores[unit][:, cols(c, BANK)],
                 in0=scores[(unit, c)][:],
@@ -281,33 +265,6 @@ def tile_gatlayer_pa_kernel(tc, q, k, h, w_v, adj, out):
                 op0=ALU.mult,
                 op1=ALU.min,
                 accum_out=minima[unit][:, c : c + 1],
-            )
-
-        def mask_by_vector(unit, c):
-            i = unit // HEADS
-            nc.vector.scalar_tensor_tensor(
-                out=neg_scores[unit][:, cols(c, BANK)],
-                in0=scores[(unit, c)][:],
-                scalar=-SCALE,
-                in1=penalty_v[i][:],
-                op0=ALU.mult,
-                op1=ALU.add,
-            )
-
-        def empty_bank(unit, c):
-            if c == BANK_ORDER[0]:
-                x = work.tile([P, NODES], F32)
-                neg_scores[unit] = x
-                mins = work.tile([P, SCORE_BANKS], F32)
-                minima[unit] = mins
-            if c < TENSOR_BANKS:
-                scale_masked(unit, c)
-            else:
-                mask_by_vector(unit, c)
-
-        def bank_minimum(unit, c):
-            nc.vector.tensor_reduce(
-                out=minima[unit][:, c : c + 1], in_=neg_scores[unit][:, cols(c, BANK)], axis=AXIS.X, op=ALU.min
             )
 
         def row_minimum(unit):
@@ -400,23 +357,17 @@ def tile_gatlayer_pa_kernel(tc, q, k, h, w_v, adj, out):
                 finish_rows(i - 2)
             if 0 <= n - 1 < UNITS:
                 exponentials(n - 1)
-            for place, c in enumerate(BANK_ORDER):
+            for c in range(SCORE_BANKS):
                 if n < UNITS:
                     empty_bank(n, c)
                 if n + 1 < UNITS:
                     score_matmul(n + 1, c)
-                if place < 2 and 0 <= n - 2 < UNITS:
-                    flip_weights(n - 2, place)
-                if place == 2 and 0 <= n - 4 < UNITS:
+                if c < 2 and 0 <= n - 2 < UNITS:
+                    flip_weights(n - 2, c)
+                if c == 2 and 0 <= n - 4 < UNITS:
                     aggregate(n - 4)
             if n == 0:
                 project_values()
-            if n < UNITS:
-                bank_minimum(n, TENSOR_BANKS)
-            if 0 <= n - 3 < UNITS:
-                quantise(n - 3)
-            if n < UNITS:
-                row_minimum(n)
             if head == 0 and i + 1 < ROW_TILES:
                 if i >= 1:
                     keep_queries(i + 1)
@@ -429,9 +380,13 @@ def tile_gatlayer_pa_kernel(tc, q, k, h, w_v, adj, out):
             if head == 2 and i + 1 < ROW_TILES:
                 keep_edges(i + 1, 4)
                 penalty_for_tensor(i + 1, 2)
-                penalty_for_vector(i + 1)
+                penalty_for_tensor(i + 1, 3)
             if head == 3 and i + 2 < ROW_TILES:
                 flip_queries(i + 2)
+            if 0 <= n - 3 < UNITS:
+                quantise(n - 3)
+            if n < UNITS:
+                row_minimum(n)
             for half in range(2):
                 if 0 <= n - 2 < UNITS:
                     group_weights(n - 2, half)
@@ -445,10 +400,9 @@ def tile_gatlayer_pa_kernel(tc, q, k, h, w_v, adj, out):
         keep_edges(0, 0)
         flip_edges(0, 4)
         keep_edges(0, 4)
-        for g in range(TENSOR_BANKS):
+        for g in range(SCORE_BANKS):
             penalty_for_tensor(0, g)
-        penalty_for_vector(0)
-        for c in BANK_ORDER:
+        for c in range(SCORE_BANKS):
             score_matmul(0, c)
         flip_keys(1)
         flip_queries(1)

@@ -239,6 +239,11 @@ def tile_gatlayer_pa_kernel(tc, q, k, h, w_v, adj, out):
                 start=True,
                 stop=False,
             )
+            scores[(unit, c)] = s_bank
+
+        def add_penalty(unit, c):
+            i = unit // HEADS
+            s_bank = scores[(unit, c)]
             for t in range(BANK // P):
                 b, m = divmod(t, 2)
                 nc.tensor.matmul(
@@ -249,7 +254,12 @@ def tile_gatlayer_pa_kernel(tc, q, k, h, w_v, adj, out):
                     stop=(t == BANK // P - 1),
                     is_transpose=True,
                 )
-            scores[(unit, c)] = s_bank
+
+        def score_pair(unit, pair):
+            for c in (2 * pair, 2 * pair + 1):
+                score_matmul(unit, c)
+            for c in (2 * pair, 2 * pair + 1):
+                add_penalty(unit, c)
 
         def empty_bank(unit, c):
             if c == 0:
@@ -357,15 +367,17 @@ def tile_gatlayer_pa_kernel(tc, q, k, h, w_v, adj, out):
                 finish_rows(i - 2)
             if 0 <= n - 1 < UNITS:
                 exponentials(n - 1)
-            for c in range(SCORE_BANKS):
+            if 0 <= n - 4 < UNITS:
+                aggregate(n - 4)
+            for pair in range(SCORE_BANKS // 2):
                 if n < UNITS:
-                    empty_bank(n, c)
+                    empty_bank(n, 2 * pair)
+                    empty_bank(n, 2 * pair + 1)
                 if n + 1 < UNITS:
-                    score_matmul(n + 1, c)
-                if c < 2 and 0 <= n - 2 < UNITS:
-                    flip_weights(n - 2, c)
-                if c == 2 and 0 <= n - 4 < UNITS:
-                    aggregate(n - 4)
+                    score_pair(n + 1, pair)
+                if pair == 0 and 0 <= n - 2 < UNITS:
+                    for half in range(2):
+                        flip_weights(n - 2, half)
             if n == 0:
                 project_values()
             if head == 0 and i + 1 < ROW_TILES:
@@ -402,8 +414,8 @@ def tile_gatlayer_pa_kernel(tc, q, k, h, w_v, adj, out):
         keep_edges(0, 4)
         for g in range(SCORE_BANKS):
             penalty_for_tensor(0, g)
-        for c in range(SCORE_BANKS):
-            score_matmul(0, c)
+        for pair in range(SCORE_BANKS // 2):
+            score_pair(0, pair)
         flip_keys(1)
         flip_queries(1)
         keep_queries(1)

@@ -27,6 +27,8 @@ ROW_TILES = NODES // P
 UNITS = ROW_TILES * HEADS
 SCORE_BANKS = NODES // BANK
 NODE_PASSES = NODES // K_PASS
+FIRST_PAIR = (0, 1)
+SECOND_PAIR = (2, 3)
 CHUNKS = NODES // (2 * P)
 SCALE = 1.0 / math.sqrt(HEAD_DIM)
 HUGE = 3.0e38
@@ -229,37 +231,49 @@ def tile_gatlayer_pa_kernel(tc, q, k, h, w_v, adj, out):
             copy_flipped(i == 0, q_t[:], q_in_psum[i][:])
             q_flipped[i] = q_t
 
-        def score_matmul(unit, c):
+        def score_matmul(unit, c, opens):
             i, head = divmod(unit, HEADS)
-            s_bank = ps_prod.tile([P, BANK], F32, tag="prod")
             nc.tensor.matmul(
-                out=s_bank[:],
+                out=scores[(unit, c)][:],
                 lhsT=q_flipped[i][:, cols(head, P)],
                 rhs=k_flipped[:, head, cols(c, BANK)],
-                start=True,
-                stop=False,
+                start=opens,
+                stop=not opens,
             )
-            scores[(unit, c)] = s_bank
 
-        def add_penalty(unit, c):
+        def add_penalty(unit, c, opens):
             i = unit // HEADS
-            s_bank = scores[(unit, c)]
             for t in range(BANK // P):
                 b, m = divmod(t, 2)
                 nc.tensor.matmul(
-                    out=s_bank[:, cols(t, P)],
+                    out=scores[(unit, c)][:, cols(t, P)],
                     lhsT=penalty_t[i][:, c, m, b, :],
                     rhs=ident_f32[:],
-                    start=False,
-                    stop=(t == BANK // P - 1),
+                    start=opens and t == 0,
+                    stop=not opens and t == BANK // P - 1,
                     is_transpose=True,
                 )
 
-        def score_pair(unit, pair):
-            for c in (2 * pair, 2 * pair + 1):
-                score_matmul(unit, c)
-            for c in (2 * pair, 2 * pair + 1):
-                add_penalty(unit, c)
+        def new_banks(unit, pair):
+            for c in pair:
+                s_bank = ps_prod.tile([P, BANK], F32, tag="prod")
+                scores[(unit, c)] = s_bank
+
+        def score_first_pair(unit):
+            new_banks(unit, FIRST_PAIR)
+            for c in FIRST_PAIR:
+                score_matmul(unit, c, opens=True)
+            for c in FIRST_PAIR:
+                add_penalty(unit, c, opens=False)
+
+        def penalty_of_second_pair(unit):
+            new_banks(unit, SECOND_PAIR)
+            for c in SECOND_PAIR:
+                add_penalty(unit, c, opens=True)
+
+        def score_second_pair(unit):
+            for c in SECOND_PAIR:
+                score_matmul(unit, c, opens=False)
 
         def empty_bank(unit, c):
             if c == 0:
@@ -363,21 +377,23 @@ def tile_gatlayer_pa_kernel(tc, q, k, h, w_v, adj, out):
                 load_rows(i + 2)
             if head == 2 and i >= 1 and i - 1 < ROW_TILES:
                 invert_row_sums(i - 1)
-            if head == 0 and i >= 2:
-                finish_rows(i - 2)
             if 0 <= n - 1 < UNITS:
                 exponentials(n - 1)
-            if 0 <= n - 4 < UNITS:
-                aggregate(n - 4)
-            for pair in range(SCORE_BANKS // 2):
-                if n < UNITS:
-                    empty_bank(n, 2 * pair)
-                    empty_bank(n, 2 * pair + 1)
-                if n + 1 < UNITS:
-                    score_pair(n + 1, pair)
-                if pair == 0 and 0 <= n - 2 < UNITS:
-                    for half in range(2):
-                        flip_weights(n - 2, half)
+            if head == 0 and i >= 2:
+                finish_rows(i - 2)
+            if n < UNITS:
+                for c in FIRST_PAIR:
+                    empty_bank(n, c)
+            if n + 1 < UNITS:
+                score_first_pair(n + 1)
+            if 0 <= n - 2 < UNITS:
+                for half in range(2):
+                    flip_weights(n - 2, half)
+            if n < UNITS:
+                for c in SECOND_PAIR:
+                    empty_bank(n, c)
+            if n + 1 < UNITS:
+                penalty_of_second_pair(n + 1)
             if n == 0:
                 project_values()
             if head == 0 and i + 1 < ROW_TILES:
@@ -395,6 +411,10 @@ def tile_gatlayer_pa_kernel(tc, q, k, h, w_v, adj, out):
                 penalty_for_tensor(i + 1, 3)
             if head == 3 and i + 2 < ROW_TILES:
                 flip_queries(i + 2)
+            if n + 1 < UNITS:
+                score_second_pair(n + 1)
+            if 0 <= n - 4 < UNITS:
+                aggregate(n - 4)
             if 0 <= n - 3 < UNITS:
                 quantise(n - 3)
             if n < UNITS:
@@ -414,8 +434,9 @@ def tile_gatlayer_pa_kernel(tc, q, k, h, w_v, adj, out):
         keep_edges(0, 4)
         for g in range(SCORE_BANKS):
             penalty_for_tensor(0, g)
-        for pair in range(SCORE_BANKS // 2):
-            score_pair(0, pair)
+        score_first_pair(0)
+        penalty_of_second_pair(0)
+        score_second_pair(0)
         flip_keys(1)
         flip_queries(1)
         keep_queries(1)

@@ -377,10 +377,13 @@ def tile_gatlayer_pa_kernel(tc, q, k, h, w_v, adj, out):
                 load_rows(i + 2)
             if head == 2 and i >= 1 and i - 1 < ROW_TILES:
                 invert_row_sums(i - 1)
-            if 0 <= n - 1 < UNITS:
-                exponentials(n - 1)
+            if 0 <= n - 3 < UNITS:
+                for half in range(2):
+                    group_weights(n - 3, half)
             if head == 0 and i >= 2:
                 finish_rows(i - 2)
+            if 0 <= n - 1 < UNITS:
+                exponentials(n - 1)
             if n < UNITS:
                 for c in FIRST_PAIR:
                     empty_bank(n, c)
@@ -419,9 +422,6 @@ def tile_gatlayer_pa_kernel(tc, q, k, h, w_v, adj, out):
                 quantise(n - 3)
             if n < UNITS:
                 row_minimum(n)
-            for half in range(2):
-                if 0 <= n - 2 < UNITS:
-                    group_weights(n - 2, half)
             if n + 2 < HEADS:
                 flip_keys(n + 2)
 

@@ -30,6 +30,7 @@ NODE_PASSES = NODES // K_PASS
 FIRST_PAIR = (0, 1)
 SECOND_PAIR = (2, 3)
 CHUNKS = NODES // (2 * P)
+LAG = 6
 SCALE = 1.0 / math.sqrt(HEAD_DIM)
 HUGE = 3.0e38
 
@@ -43,9 +44,10 @@ def tile_gatlayer_pa_kernel(tc, q, k, h, w_v, adj, out):
     with ExitStack() as ctx:
         const = ctx.enter_context(tc.tile_pool(name="const", bufs=1))
         keep = ctx.enter_context(tc.tile_pool(name="keep", bufs=1))
-        stage = ctx.enter_context(tc.tile_pool(name="stage", bufs=2))
+        stage = ctx.enter_context(tc.tile_pool(name="stage", bufs=4))
         rows = ctx.enter_context(tc.tile_pool(name="rows", bufs=2))
         work = ctx.enter_context(tc.tile_pool(name="work", bufs=3))
+        codes = ctx.enter_context(tc.tile_pool(name="codes", bufs=LAG))
         ps_prod = ctx.enter_context(tc.psum_pool(name="ps_prod", bufs=4))
         ps_flip = ctx.enter_context(tc.psum_pool(name="ps_flip", bufs=2))
         ps_out = ctx.enter_context(tc.psum_pool(name="ps_out", bufs=1))
@@ -56,26 +58,19 @@ def tile_gatlayer_pa_kernel(tc, q, k, h, w_v, adj, out):
         ident_bf16 = const.tile([P, P], BF16)
         make_identity(nc, ident_bf16[:])
 
-        def regroup(grouped, by_row):
-            nc.gpsimd.tensor_scalar(
-                out=grouped[:].rearrange("p (c t) -> p c t", t=PACK),
-                in0=by_row[:].rearrange("p t c -> p c t"),
-                scalar1=1.0,
-                scalar2=0.0,
-                op0=ALU.mult,
-                op1=ALU.add,
-            )
+        def grouped_view(grouped):
+            return grouped.rearrange("p (c t) -> p c t", t=PACK)
 
         q_rows = {}
         adj_rows = {}
 
         def load_rows(i):
-            q_tile = rows.tile([P, HEADS, HEAD_DIM], BF16)
-            nc.sync.dma_start(out=q_tile[:], in_=q[0, :, cols(i, P), :].rearrange("n p d -> p n d"))
-            q_rows[i] = q_tile
             adj_tile = rows.tile([P, NODES], BF16)
             nc.sync.dma_start(out=adj_tile[:], in_=adj[cols(i, P), :])
             adj_rows[i] = adj_tile
+            q_tile = rows.tile([P, HEADS, HEAD_DIM], BF16)
+            nc.sync.dma_start(out=q_tile[:], in_=q[0, :, cols(i, P), :].rearrange("n p d -> p n d"))
+            q_rows[i] = q_tile
 
         k_rows = keep.tile([P, HEADS, ROW_TILES // 2, 2, HEAD_DIM], BF16)
 
@@ -84,22 +79,27 @@ def tile_gatlayer_pa_kernel(tc, q, k, h, w_v, adj, out):
                 out=k_rows[:, head, :, :, :], in_=k[0, head].rearrange("(m p b) d -> p m b d", p=P, b=2)
             )
 
-        load_keys(0)
         load_rows(0)
+        load_keys(0)
         load_keys(1)
-        load_rows(1)
         w_rows = keep.tile([P, PACK, FEATURES], BF16)
         nc.sync.dma_start(
             out=w_rows[:].rearrange("p (u b) c -> p u b c", u=2),
             in_=w_v.rearrange("(u p b) c -> p u b c", u=2, b=2),
         )
         h_rows = keep.tile([P, NODE_PASSES, PACK, FEATURES], BF16)
-        for g in range(NODE_PASSES):
+
+        def load_features(g):
             nc.sync.dma_start(
                 out=h_rows[:, g, :, :], in_=h[0, cols(g, K_PASS), :].rearrange("(p s) k -> p s k", s=PACK)
             )
+
+        for g in range(NODE_PASSES):
+            load_features(g)
         load_keys(2)
+        load_rows(1)
         load_keys(3)
+        load_rows(2)
 
         w_codes = keep.tile([P, FEATURES], U32, align_bytes=64)
         w_scales = keep.tile([P, FEATURES], U8, align_bytes=64)
@@ -108,62 +108,87 @@ def tile_gatlayer_pa_kernel(tc, q, k, h, w_v, adj, out):
         v_codes = keep.tile([P, NODE_PASSES, FEATURES], U32, align_bytes=64)
         v_scales = keep.tile([P, NODE_PASSES, FEATURES], U8, align_bytes=64)
 
+        v_grouped = keep.tile([P, NODE_PASSES, FEATURES * PACK], BF16, align_bytes=64)
+
         def shared_copy(piece, out_ap, in_ap):
-            if piece % 2 == 0:
+            if piece % 2 == 1:
                 nc.vector.tensor_copy(out=out_ap, in_=in_ap)
             else:
                 nc.scalar.copy(out=out_ap, in_=in_ap)
 
-        def project_values():
-            w_grouped = stage.tile([P, FEATURES * PACK], BF16, align_bytes=64)
-            regroup(w_grouped, w_rows)
+        w_grouped = keep.tile([P, FEATURES * PACK], BF16, align_bytes=64)
+
+        def group_w():
+            nc.vector.tensor_copy(out=grouped_view(w_grouped[:]), in_=w_rows[:].rearrange("p t c -> p c t"))
+
+        def quantise_w():
             nc.vector.quantize_mx(out=w_codes[:].bitcast(FP8X4), scales=w_scales[:], in_=w_grouped[:])
 
-            for a in range(NODES // (2 * P)):
+        h_flipped = {}
+        h_grouped = {}
+
+        def flip_h(g):
+            for u in range(2):
                 h_flip = ps_flip.tile([P, BANK], F32, tag="flip")
                 for b in range(2):
-                    h_pairs = h_rows[:, a // 2, 2 * b + a % 2, :].bitcast(F32)
-                    for u in range(2):
-                        nc.tensor.transpose(h_flip[:, cols(2 * b + u, P)], h_pairs[:, cols(u, P)], ident_f32[:])
-                h_grouped = stage.tile([P, 2 * P * PACK], BF16, align_bytes=64)
-                shared_copy(
-                    a,
-                    h_grouped[:].bitcast(F32).rearrange("p (b r u) -> p b r u", b=2, u=2),
-                    h_flip[:].rearrange("p (b u r) -> p b r u", b=2, u=2),
-                )
-                nc.vector.quantize_mx(
-                    out=h_codes[:, cols(a, 2 * P)].bitcast(FP8X4),
-                    scales=h_scales[:, cols(a, 2 * P)],
-                    in_=h_grouped[:],
-                )
+                    h_pairs = h_rows[:, g, 2 * b + u, :].bitcast(F32)
+                    for v in range(2):
+                        nc.tensor.transpose(h_flip[:, cols(2 * b + v, P)], h_pairs[:, cols(v, P)], ident_f32[:])
+                h_flipped[(g, u)] = h_flip
 
-            for g in range(NODE_PASSES):
-                v_rows = stage.tile([P, PACK, FEATURES], BF16)
-                for t in range(PACK):
-                    if t % 2 == 0:
-                        v_sum = ps_out.tile([P, BANK], F32, tag="out")
-                    else:
-                        v_sum = ps_misc.tile([P, BANK], F32, tag="misc")
-                    nc.tensor.matmul_mx(
-                        out=v_sum[:],
-                        lhsT=h_codes[:, cols(PACK * g + t, P)].bitcast(FP8X4),
-                        lhsT_scale=h_scales[:, cols(PACK * g + t, P)],
-                        rhs=w_codes[:].bitcast(FP8X4),
-                        rhs_scale=w_scales[:],
-                        start=True,
-                        stop=True,
-                    )
-                    shared_copy(t, v_rows[:, t, :], v_sum[:])
-                v_grouped = stage.tile([P, FEATURES * PACK], BF16, align_bytes=64)
-                regroup(v_grouped, v_rows)
-                nc.vector.quantize_mx(
-                    out=v_codes[:, g, :].bitcast(FP8X4), scales=v_scales[:, g, :], in_=v_grouped[:]
+        def group_h(g, u):
+            grouped = stage.tile([P, 2 * P * PACK], BF16, align_bytes=64)
+            nc.scalar.copy(
+                out=grouped[:].bitcast(F32).rearrange("p (b r v) -> p b r v", b=2, v=2),
+                in_=h_flipped[(g, u)][:].rearrange("p (b v r) -> p b r v", b=2, v=2),
+            )
+            h_grouped[(g, u)] = grouped
+
+        def quantise_h(g, u):
+            a = 2 * g + u
+            nc.vector.quantize_mx(
+                out=h_codes[:, cols(a, 2 * P)].bitcast(FP8X4),
+                scales=h_scales[:, cols(a, 2 * P)],
+                in_=h_grouped[(g, u)][:],
+            )
+
+        def project(g):
+            v_rows = stage.tile([P, PACK, FEATURES], BF16)
+            for t in range(PACK):
+                if t < 2:
+                    v_sum = ps_flip.tile([P, BANK], F32, tag="flip")
+                elif t == 2:
+                    v_sum = ps_out.tile([P, BANK], F32, tag="out")
+                else:
+                    v_sum = ps_misc.tile([P, BANK], F32, tag="misc")
+                nc.tensor.matmul_mx(
+                    out=v_sum[:],
+                    lhsT=h_codes[:, cols(PACK * g + t, P)].bitcast(FP8X4),
+                    lhsT_scale=h_scales[:, cols(PACK * g + t, P)],
+                    rhs=w_codes[:].bitcast(FP8X4),
+                    rhs_scale=w_scales[:],
+                    start=True,
+                    stop=True,
                 )
+                shared_copy(t, v_rows[:, t, :], v_sum[:])
+            nc.gpsimd.tensor_scalar(
+                out=grouped_view(v_grouped[:, g, :]),
+                in0=v_rows[:].rearrange("p t c -> p c t"),
+                scalar1=1.0,
+                scalar2=0.0,
+                op0=ALU.mult,
+                op1=ALU.add,
+            )
+
+        def quantise_v(g):
+            nc.vector.quantize_mx(
+                out=v_codes[:, g, :].bitcast(FP8X4), scales=v_scales[:, g, :], in_=v_grouped[:, g, :]
+            )
 
         k_flipped = keep.tile([P, HEADS, NODES], BF16)
 
-        def copy_flipped(first, out_ap, in_ap):
-            if first:
+        def copy_flipped(by_vector, out_ap, in_ap):
+            if by_vector:
                 nc.vector.tensor_copy(out=out_ap, in_=in_ap)
             else:
                 nc.scalar.copy(out=out_ap, in_=in_ap)
@@ -174,7 +199,7 @@ def tile_gatlayer_pa_kernel(tc, q, k, h, w_v, adj, out):
                 for t in range(BANK // P):
                     b, m = divmod(t, 2)
                     nc.tensor.transpose(k_flip[:, cols(t, P)], k_rows[:, head, 2 * c + m, b, :], ident_bf16[:])
-                copy_flipped(head == 0, k_flipped[:, head, cols(c, BANK)], k_flip[:])
+                copy_flipped(c % 2 == 0 and head < 2, k_flipped[:, head, cols(c, BANK)], k_flip[:])
 
         edges_in_psum = {}
         edges_flipped = {}
@@ -195,7 +220,10 @@ def tile_gatlayer_pa_kernel(tc, q, k, h, w_v, adj, out):
 
         def flip_edges(i, first):
             words = adj_rows[i][:].bitcast(F32)
-            bank = ps_misc.tile([P, BANK], F32, tag="misc")
+            if i == 0 and first > 0:
+                bank = ps_out.tile([P, BANK], F32, tag="out")
+            else:
+                bank = ps_misc.tile([P, BANK], F32, tag="misc")
             for c in range(first, first + 4):
                 nc.tensor.transpose(bank[:, cols(c - first, P)], words[:, cols(c, P)], ident_f32[:])
             edges_in_psum[(i, first)] = bank
@@ -204,7 +232,11 @@ def tile_gatlayer_pa_kernel(tc, q, k, h, w_v, adj, out):
             if first == 0:
                 flipped = rows.tile([P, CHUNKS * P], F32)
                 edges_flipped[i] = flipped
-            nc.vector.tensor_copy(out=edges_flipped[i][:, cols(first // 4, BANK)], in_=edges_in_psum[(i, first)][:])
+            out_ap = edges_flipped[i][:, cols(first // 4, BANK)]
+            if i == 0 and first > 0:
+                nc.scalar.copy(out=out_ap, in_=edges_in_psum[(i, first)][:])
+            else:
+                nc.vector.tensor_copy(out=out_ap, in_=edges_in_psum[(i, first)][:])
 
         def penalty_for_tensor(i, g):
             if g == 0:
@@ -263,7 +295,7 @@ def tile_gatlayer_pa_kernel(tc, q, k, h, w_v, adj, out):
             new_banks(unit, FIRST_PAIR)
             for c in FIRST_PAIR:
                 score_matmul(unit, c, opens=True)
-            for c in FIRST_PAIR:
+            for c in reversed(FIRST_PAIR):
                 add_penalty(unit, c, opens=False)
 
         def penalty_of_second_pair(unit):
@@ -272,7 +304,7 @@ def tile_gatlayer_pa_kernel(tc, q, k, h, w_v, adj, out):
                 add_penalty(unit, c, opens=True)
 
         def score_second_pair(unit):
-            for c in SECOND_PAIR:
+            for c in reversed(SECOND_PAIR):
                 score_matmul(unit, c, opens=False)
 
         def empty_bank(unit, c):
@@ -332,8 +364,8 @@ def tile_gatlayer_pa_kernel(tc, q, k, h, w_v, adj, out):
             )
 
         def quantise(unit):
-            e_codes = work.tile([P, NODE_PASSES * P], U32, align_bytes=64)
-            e_scales = work.tile([P, NODE_PASSES * P], U8, align_bytes=64)
+            e_codes = codes.tile([P, NODE_PASSES * P], U32, align_bytes=64)
+            e_scales = codes.tile([P, NODE_PASSES * P], U8, align_bytes=64)
             nc.vector.quantize_mx(out=e_codes[:].bitcast(FP8X4), scales=e_scales[:], in_=e_grouped[unit][:])
             e_quantised[unit] = (e_codes, e_scales)
 
@@ -373,14 +405,19 @@ def tile_gatlayer_pa_kernel(tc, q, k, h, w_v, adj, out):
 
         def step(n):
             i, head = divmod(n, HEADS)
+            more_rows = i + 1 < ROW_TILES
             if head == 0 and i + 2 < ROW_TILES:
                 load_rows(i + 2)
-            if head == 2 and i >= 1 and i - 1 < ROW_TILES:
+            if head == 1 and 1 <= i <= ROW_TILES:
                 invert_row_sums(i - 1)
             if 0 <= n - 3 < UNITS:
                 for half in range(2):
                     group_weights(n - 3, half)
-            if head == 0 and i >= 2:
+            if n == 3:
+                keep_queries(1)
+            if head == 0 and more_rows:
+                keep_queries(i + 1)
+            if head == 2 and i >= 2:
                 finish_rows(i - 2)
             if 0 <= n - 1 < UNITS:
                 exponentials(n - 1)
@@ -390,59 +427,86 @@ def tile_gatlayer_pa_kernel(tc, q, k, h, w_v, adj, out):
             if n + 1 < UNITS:
                 score_first_pair(n + 1)
             if 0 <= n - 2 < UNITS:
-                for half in range(2):
+                for half in reversed(range(2)):
                     flip_weights(n - 2, half)
             if n < UNITS:
                 for c in SECOND_PAIR:
                     empty_bank(n, c)
             if n + 1 < UNITS:
                 penalty_of_second_pair(n + 1)
-            if n == 0:
-                project_values()
-            if head == 0 and i + 1 < ROW_TILES:
-                if i >= 1:
-                    keep_queries(i + 1)
+            if head == 0 and more_rows:
                 flip_edges(i + 1, 0)
-            if head == 1 and i + 1 < ROW_TILES:
+            if head == 1 and more_rows:
                 keep_edges(i + 1, 0)
                 flip_edges(i + 1, 4)
                 penalty_for_tensor(i + 1, 0)
                 penalty_for_tensor(i + 1, 1)
-            if head == 2 and i + 1 < ROW_TILES:
+            if head == 2 and more_rows:
                 keep_edges(i + 1, 4)
                 penalty_for_tensor(i + 1, 2)
                 penalty_for_tensor(i + 1, 3)
+            if n == 2:
+                flip_queries(1)
             if head == 3 and i + 2 < ROW_TILES:
                 flip_queries(i + 2)
             if n + 1 < UNITS:
                 score_second_pair(n + 1)
-            if 0 <= n - 4 < UNITS:
-                aggregate(n - 4)
+            if 0 <= n - LAG < UNITS:
+                aggregate(n - LAG)
+            if n == 1:
+                flip_keys(3)
+            if 0 <= n - 2 < NODE_PASSES:
+                quantise_v(n - 2)
             if 0 <= n - 3 < UNITS:
                 quantise(n - 3)
             if n < UNITS:
                 row_minimum(n)
-            if n + 2 < HEADS:
-                flip_keys(n + 2)
 
-        flip_keys(0)
-        flip_queries(0)
-        keep_queries(0)
-        flip_edges(0, 0)
-        keep_edges(0, 0)
-        flip_edges(0, 4)
-        keep_edges(0, 4)
-        for g in range(SCORE_BANKS):
-            penalty_for_tensor(0, g)
-        score_first_pair(0)
-        penalty_of_second_pair(0)
-        score_second_pair(0)
-        flip_keys(1)
-        flip_queries(1)
-        keep_queries(1)
-        for n in range(HEADS):
-            step(n)
+        def first_step():
+            flip_edges(0, 0)
+            flip_edges(0, 4)
+            keep_edges(0, 0)
+            keep_edges(0, 4)
+            for g in range(SCORE_BANKS):
+                penalty_for_tensor(0, g)
+            flip_queries(0)
+            keep_queries(0)
+            flip_keys(0)
+            flip_keys(1)
+            group_w()
+            score_first_pair(0)
+            penalty_of_second_pair(0)
+            score_second_pair(0)
+            for g in range(2):
+                flip_h(g)
+                for u in range(2):
+                    group_h(g, u)
+            for c in FIRST_PAIR:
+                empty_bank(0, c)
+            quantise_w()
+            score_first_pair(1)
+            for g in range(2):
+                for u in range(2):
+                    quantise_h(g, u)
+            for g in range(2, NODE_PASSES):
+                flip_h(g)
+                for u in range(2):
+                    group_h(g, u)
+            for c in SECOND_PAIR:
+                empty_bank(0, c)
+            penalty_of_second_pair(1)
+            score_second_pair(1)
+            for g in range(2, NODE_PASSES):
+                for u in range(2):
+                    quantise_h(g, u)
+            row_minimum(0)
+            flip_keys(2)
+            for g in range(NODE_PASSES):
+                project(g)
+            flip_edges(1, 0)
+
         with tc.manual_schedule():
-            for n in range(HEADS, UNITS + 4):
+            first_step()
+            for n in range(1, UNITS + LAG):
                 step(n)
             finish_rows(ROW_TILES - 1)

@@ -29,8 +29,10 @@ SCORE_BANKS = NODES // BANK
 NODE_PASSES = NODES // K_PASS
 FIRST_PAIR = (0, 1)
 SECOND_PAIR = (2, 3)
+EARLY_ROWS = 2
 CHUNKS = NODES // (2 * P)
 LAG = 6
+LATE = 3
 SCALE = 1.0 / math.sqrt(HEAD_DIM)
 HUGE = 3.0e38
 
@@ -99,7 +101,6 @@ def tile_gatlayer_pa_kernel(tc, q, k, h, w_v, adj, out):
         load_keys(2)
         load_rows(1)
         load_keys(3)
-        load_rows(2)
 
         w_codes = keep.tile([P, FEATURES], U32, align_bytes=64)
         w_scales = keep.tile([P, FEATURES], U8, align_bytes=64)
@@ -129,7 +130,7 @@ def tile_gatlayer_pa_kernel(tc, q, k, h, w_v, adj, out):
 
         def flip_h(g):
             for u in range(2):
-                h_flip = ps_flip.tile([P, BANK], F32, tag="flip")
+                h_flip = spare_bank(2 * (g % 2) + u, F32)
                 for b in range(2):
                     h_pairs = h_rows[:, g, 2 * b + u, :].bitcast(F32)
                     for v in range(2):
@@ -152,15 +153,12 @@ def tile_gatlayer_pa_kernel(tc, q, k, h, w_v, adj, out):
                 in_=h_grouped[(g, u)][:],
             )
 
-        def project(g):
-            v_rows = stage.tile([P, PACK, FEATURES], BF16)
+        v_sums = {}
+
+        def multiply_h(g):
             for t in range(PACK):
-                if t < 2:
-                    v_sum = ps_flip.tile([P, BANK], F32, tag="flip")
-                elif t == 2:
-                    v_sum = ps_out.tile([P, BANK], F32, tag="out")
-                else:
-                    v_sum = ps_misc.tile([P, BANK], F32, tag="misc")
+                v_sum = spare_bank(t, F32)
+                v_sums[(g, t)] = v_sum
                 nc.tensor.matmul_mx(
                     out=v_sum[:],
                     lhsT=h_codes[:, cols(PACK * g + t, P)].bitcast(FP8X4),
@@ -170,7 +168,11 @@ def tile_gatlayer_pa_kernel(tc, q, k, h, w_v, adj, out):
                     start=True,
                     stop=True,
                 )
-                shared_copy(t, v_rows[:, t, :], v_sum[:])
+
+        def group_v(g):
+            v_rows = stage.tile([P, PACK, FEATURES], BF16)
+            for t in range(PACK):
+                shared_copy(1 if t == 3 else 0, v_rows[:, t, :], v_sums[(g, t)][:])
             nc.gpsimd.tensor_scalar(
                 out=grouped_view(v_grouped[:, g, :]),
                 in0=v_rows[:].rearrange("p t c -> p c t"),
@@ -193,17 +195,27 @@ def tile_gatlayer_pa_kernel(tc, q, k, h, w_v, adj, out):
             else:
                 nc.scalar.copy(out=out_ap, in_=in_ap)
 
+        def spare_bank(place, dtype):
+            if place == 2:
+                bank = ps_out.tile([P, BANK], dtype, tag="out")
+            elif place == 3:
+                bank = ps_misc.tile([P, BANK], dtype, tag="misc")
+            else:
+                bank = ps_flip.tile([P, BANK], dtype, tag="flip")
+            return bank
+
         def flip_keys(head):
             for c in range(SCORE_BANKS):
-                k_flip = ps_flip.tile([P, BANK], BF16, tag="flip")
+                k_flip = spare_bank(c if head < 3 else 0, BF16)
                 for t in range(BANK // P):
                     b, m = divmod(t, 2)
                     nc.tensor.transpose(k_flip[:, cols(t, P)], k_rows[:, head, 2 * c + m, b, :], ident_bf16[:])
-                copy_flipped(c % 2 == 0 and head < 2, k_flipped[:, head, cols(c, BANK)], k_flip[:])
+                copy_flipped(head == 2 or (c % 2 == 0 and head < 2), k_flipped[:, head, cols(c, BANK)], k_flip[:])
 
         edges_in_psum = {}
         edges_flipped = {}
         penalty_t = {}
+        penalty_n = {}
         minima = {}
         q_in_psum = {}
         q_flipped = {}
@@ -220,10 +232,7 @@ def tile_gatlayer_pa_kernel(tc, q, k, h, w_v, adj, out):
 
         def flip_edges(i, first):
             words = adj_rows[i][:].bitcast(F32)
-            if i == 0 and first > 0:
-                bank = ps_out.tile([P, BANK], F32, tag="out")
-            else:
-                bank = ps_misc.tile([P, BANK], F32, tag="misc")
+            bank = ps_misc.tile([P, BANK], F32, tag="misc")
             for c in range(first, first + 4):
                 nc.tensor.transpose(bank[:, cols(c - first, P)], words[:, cols(c, P)], ident_f32[:])
             edges_in_psum[(i, first)] = bank
@@ -232,11 +241,7 @@ def tile_gatlayer_pa_kernel(tc, q, k, h, w_v, adj, out):
             if first == 0:
                 flipped = rows.tile([P, CHUNKS * P], F32)
                 edges_flipped[i] = flipped
-            out_ap = edges_flipped[i][:, cols(first // 4, BANK)]
-            if i == 0 and first > 0:
-                nc.scalar.copy(out=out_ap, in_=edges_in_psum[(i, first)][:])
-            else:
-                nc.vector.tensor_copy(out=out_ap, in_=edges_in_psum[(i, first)][:])
+            nc.vector.tensor_copy(out=edges_flipped[i][:, cols(first // 4, BANK)], in_=edges_in_psum[(i, first)][:])
 
         def penalty_for_tensor(i, g):
             if g == 0:
@@ -251,6 +256,19 @@ def tile_gatlayer_pa_kernel(tc, q, k, h, w_v, adj, out):
                 op0=ALU.mult,
                 op1=ALU.add,
             )
+
+        def penalty_early(i):
+            pen = rows.tile([P, NODES], BF16)
+            for g in range(SCORE_BANKS):
+                nc.gpsimd.tensor_scalar(
+                    out=pen[:, cols(g, BANK)].rearrange("p (b y) -> p b y", b=2),
+                    in0=adj_rows[i][:, cols(g, BANK)].rearrange("p (y b) -> p b y", b=2),
+                    scalar1=HUGE,
+                    scalar2=-HUGE,
+                    op0=ALU.mult,
+                    op1=ALU.add,
+                )
+            penalty_n[i] = pen
 
         def flip_queries(i):
             q_flip = ps_misc.tile([P, BANK], BF16, tag="misc")
@@ -286,12 +304,30 @@ def tile_gatlayer_pa_kernel(tc, q, k, h, w_v, adj, out):
                     is_transpose=True,
                 )
 
+        def add_penalty_early(unit, c):
+            nc.tensor.matmul(
+                out=scores[(unit, c)][:],
+                lhsT=ident_bf16[:],
+                rhs=penalty_n[unit // HEADS][:, cols(c, BANK)],
+                start=False,
+                stop=True,
+            )
+
+        def score_early(unit, pair):
+            new_banks(unit, pair)
+            for c in reversed(pair):
+                score_matmul(unit, c, opens=True)
+                add_penalty_early(unit, c)
+
         def new_banks(unit, pair):
             for c in pair:
                 s_bank = ps_prod.tile([P, BANK], F32, tag="prod")
                 scores[(unit, c)] = s_bank
 
         def score_first_pair(unit):
+            if unit < EARLY_ROWS * HEADS:
+                score_early(unit, FIRST_PAIR)
+                return
             new_banks(unit, FIRST_PAIR)
             for c in FIRST_PAIR:
                 score_matmul(unit, c, opens=True)
@@ -299,11 +335,16 @@ def tile_gatlayer_pa_kernel(tc, q, k, h, w_v, adj, out):
                 add_penalty(unit, c, opens=False)
 
         def penalty_of_second_pair(unit):
+            if unit < EARLY_ROWS * HEADS:
+                return
             new_banks(unit, SECOND_PAIR)
             for c in SECOND_PAIR:
                 add_penalty(unit, c, opens=True)
 
         def score_second_pair(unit):
+            if unit < EARLY_ROWS * HEADS:
+                score_early(unit, SECOND_PAIR)
+                return
             for c in reversed(SECOND_PAIR):
                 score_matmul(unit, c, opens=False)
 
@@ -353,15 +394,17 @@ def tile_gatlayer_pa_kernel(tc, q, k, h, w_v, adj, out):
                 )
             e_flipped[(unit, half)] = e_flip
 
-        def group_weights(unit, half):
+        def group_weights(unit, half, by_vector=False):
             if half == 0:
                 grouped = work.tile([P, NODE_PASSES * P * PACK], BF16, align_bytes=64)
                 e_grouped[unit] = grouped
             grouped_pairs = e_grouped[unit][:].bitcast(F32).rearrange("p (g r u) -> p g r u", r=P, u=2)
-            nc.scalar.copy(
-                out=grouped_pairs[:, cols(half, 2), :, :],
-                in_=e_flipped[(unit, half)][:].rearrange("p (g u r) -> p g r u", g=2, u=2),
-            )
+            out_ap = grouped_pairs[:, cols(half, 2), :, :]
+            in_ap = e_flipped[(unit, half)][:].rearrange("p (g u r) -> p g r u", g=2, u=2)
+            if by_vector:
+                nc.vector.tensor_copy(out=out_ap, in_=in_ap)
+            else:
+                nc.scalar.copy(out=out_ap, in_=in_ap)
 
         def quantise(unit):
             e_codes = codes.tile([P, NODE_PASSES * P], U32, align_bytes=64)
@@ -392,121 +435,148 @@ def tile_gatlayer_pa_kernel(tc, q, k, h, w_v, adj, out):
             inverse_sum[i] = inverse
 
         def finish_rows(i):
-            inverse = inverse_sum[i]
+            sums = rows.tile([P, FEATURES], F32)
+            nc.scalar.copy(out=sums[:], in_=out_sum[i][:])
             result = rows.tile([P, FEATURES], F32)
             for head in range(HEADS):
-                nc.scalar.activation(
+                nc.gpsimd.tensor_scalar(
                     out=result[:, cols(head, HEAD_DIM)],
-                    in_=out_sum[i][:, cols(head, HEAD_DIM)],
-                    func=ACT.Copy,
-                    scale=inverse[:, head : head + 1],
+                    in0=sums[:, cols(head, HEAD_DIM)],
+                    scalar1=inverse_sum[i][:, head : head + 1],
+                    scalar2=0.0,
+                    op0=ALU.mult,
+                    op1=ALU.add,
                 )
             nc.sync.dma_start(out=out[0, cols(i, P), :], in_=result[:])
 
+        def finish_head(i, head):
+            result = rows.tile([P, HEAD_DIM], F32)
+            nc.scalar.activation(
+                out=result[:],
+                in_=out_sum[i][:, cols(head, HEAD_DIM)],
+                func=ACT.Copy,
+                scale=inverse_sum[i][:, head : head + 1],
+            )
+            nc.sync.dma_start(out=out[0, cols(i, P), cols(head, HEAD_DIM)], in_=result[:])
+
         def step(n):
             i, head = divmod(n, HEADS)
-            more_rows = i + 1 < ROW_TILES
+            next_edges = EARLY_ROWS <= i + 1 < ROW_TILES
             if head == 0 and i + 2 < ROW_TILES:
                 load_rows(i + 2)
-            if head == 1 and 1 <= i <= ROW_TILES:
+            if head == 2 and 1 <= i <= ROW_TILES:
                 invert_row_sums(i - 1)
-            if 0 <= n - 3 < UNITS:
+            if 0 <= n - 3 < UNITS - LATE:
                 for half in range(2):
                     group_weights(n - 3, half)
-            if n == 3:
-                keep_queries(1)
-            if head == 0 and more_rows:
+            if head == 0 and i + 1 < ROW_TILES:
                 keep_queries(i + 1)
-            if head == 2 and i >= 2:
-                finish_rows(i - 2)
-            if 0 <= n - 1 < UNITS:
-                exponentials(n - 1)
             if n < UNITS:
-                for c in FIRST_PAIR:
-                    empty_bank(n, c)
+                empty_bank(n, 0)
+            if n - 1 < UNITS:
+                if n > 1:
+                    row_minimum(n - 1)
+                    exponentials(n - 1)
+            if head == 2 and 2 <= i:
+                finish_rows(i - 2)
+            if n < UNITS:
+                empty_bank(n, 1)
             if n + 1 < UNITS:
                 score_first_pair(n + 1)
             if 0 <= n - 2 < UNITS:
                 for half in reversed(range(2)):
                     flip_weights(n - 2, half)
-            if n < UNITS:
-                for c in SECOND_PAIR:
-                    empty_bank(n, c)
-            if n + 1 < UNITS:
-                penalty_of_second_pair(n + 1)
-            if head == 0 and more_rows:
-                flip_edges(i + 1, 0)
-            if head == 1 and more_rows:
+            if head == 1 and next_edges:
                 keep_edges(i + 1, 0)
-                flip_edges(i + 1, 4)
                 penalty_for_tensor(i + 1, 0)
                 penalty_for_tensor(i + 1, 1)
-            if head == 2 and more_rows:
+            if head == 2 and next_edges:
                 keep_edges(i + 1, 4)
                 penalty_for_tensor(i + 1, 2)
                 penalty_for_tensor(i + 1, 3)
-            if n == 2:
-                flip_queries(1)
+            if 0 <= n - 2 < NODE_PASSES:
+                quantise_v(n - 2)
+            if 0 <= n - 4 < UNITS:
+                quantise(n - 4)
+            if n < UNITS:
+                for c in SECOND_PAIR:
+                    empty_bank(n, c)
+            if n == 1:
+                group_v(1)
+                multiply_h(2)
+                group_v(2)
+            if n + 1 < UNITS:
+                penalty_of_second_pair(n + 1)
+            if head == 0 and next_edges:
+                flip_edges(i + 1, 0)
+            if head == 1 and next_edges:
+                flip_edges(i + 1, 4)
             if head == 3 and i + 2 < ROW_TILES:
                 flip_queries(i + 2)
             if n + 1 < UNITS:
                 score_second_pair(n + 1)
             if 0 <= n - LAG < UNITS:
                 aggregate(n - LAG)
+                if n - LAG >= UNITS - HEADS:
+                    finish_head(ROW_TILES - 1, (n - LAG) % HEADS)
             if n == 1:
+                multiply_h(3)
+                group_v(3)
                 flip_keys(3)
-            if 0 <= n - 2 < NODE_PASSES:
-                quantise_v(n - 2)
-            if 0 <= n - 3 < UNITS:
-                quantise(n - 3)
-            if n < UNITS:
-                row_minimum(n)
+            if UNITS - LATE <= n - 3 < UNITS:
+                for half in range(2):
+                    group_weights(n - 3, half, by_vector=n - 3 < UNITS - 1 or half == 0)
 
         def first_step():
-            flip_edges(0, 0)
-            flip_edges(0, 4)
-            keep_edges(0, 0)
-            keep_edges(0, 4)
-            for g in range(SCORE_BANKS):
-                penalty_for_tensor(0, g)
+            penalty_early(0)
             flip_queries(0)
             keep_queries(0)
             flip_keys(0)
             flip_keys(1)
+            flip_h(0)
+            for u in range(2):
+                group_h(0, u)
             group_w()
             score_first_pair(0)
-            penalty_of_second_pair(0)
             score_second_pair(0)
-            for g in range(2):
-                flip_h(g)
-                for u in range(2):
-                    group_h(g, u)
+            flip_h(1)
+            for u in range(2):
+                group_h(1, u)
             for c in FIRST_PAIR:
                 empty_bank(0, c)
             quantise_w()
             score_first_pair(1)
-            for g in range(2):
-                for u in range(2):
-                    quantise_h(g, u)
-            for g in range(2, NODE_PASSES):
-                flip_h(g)
-                for u in range(2):
-                    group_h(g, u)
+            for u in range(2):
+                quantise_h(0, u)
+            flip_h(2)
+            for u in range(2):
+                group_h(2, u)
             for c in SECOND_PAIR:
                 empty_bank(0, c)
-            penalty_of_second_pair(1)
             score_second_pair(1)
+            for u in range(2):
+                quantise_h(1, u)
+            flip_h(3)
+            for u in range(2):
+                group_h(3, u)
+            row_minimum(0)
+            exponentials(0)
             for g in range(2, NODE_PASSES):
                 for u in range(2):
                     quantise_h(g, u)
-            row_minimum(0)
+            flip_queries(1)
+            keep_queries(1)
             flip_keys(2)
-            for g in range(NODE_PASSES):
-                project(g)
-            flip_edges(1, 0)
+            penalty_early(1)
+            multiply_h(0)
+            group_v(0)
+            multiply_h(1)
+            load_rows(2)
 
         with tc.manual_schedule():
             first_step()
-            for n in range(1, UNITS + LAG):
+            for n in range(1, UNITS + 4):
                 step(n)
-            finish_rows(ROW_TILES - 1)
+            for unit in range(UNITS + 4 - LAG, UNITS):
+                aggregate(unit)
+                finish_head(ROW_TILES - 1, unit % HEADS)

@@ -324,29 +324,23 @@ def tile_gatlayer_pa_kernel(tc, q, k, h, w_v, adj, out):
                 s_bank = ps_prod.tile([P, BANK], F32, tag="prod")
                 scores[(unit, c)] = s_bank
 
-        def score_first_pair(unit):
+        def score_pair_matmuls(unit, pair):
             if unit < EARLY_ROWS * HEADS:
-                score_early(unit, FIRST_PAIR)
+                score_early(unit, pair)
                 return
-            new_banks(unit, FIRST_PAIR)
-            for c in FIRST_PAIR:
+            new_banks(unit, pair)
+            for c in pair:
                 score_matmul(unit, c, opens=True)
-            for c in reversed(FIRST_PAIR):
+
+        def score_pair_penalty(unit, pair):
+            if unit < EARLY_ROWS * HEADS:
+                return
+            for c in reversed(pair):
                 add_penalty(unit, c, opens=False)
 
-        def penalty_of_second_pair(unit):
-            if unit < EARLY_ROWS * HEADS:
-                return
-            new_banks(unit, SECOND_PAIR)
-            for c in SECOND_PAIR:
-                add_penalty(unit, c, opens=True)
-
-        def score_second_pair(unit):
-            if unit < EARLY_ROWS * HEADS:
-                score_early(unit, SECOND_PAIR)
-                return
-            for c in reversed(SECOND_PAIR):
-                score_matmul(unit, c, opens=False)
+        def score_pair(unit, pair):
+            score_pair_matmuls(unit, pair)
+            score_pair_penalty(unit, pair)
 
         def empty_bank(unit, c):
             if c == 0:
@@ -435,17 +429,13 @@ def tile_gatlayer_pa_kernel(tc, q, k, h, w_v, adj, out):
             inverse_sum[i] = inverse
 
         def finish_rows(i):
-            sums = rows.tile([P, FEATURES], F32)
-            nc.scalar.copy(out=sums[:], in_=out_sum[i][:])
             result = rows.tile([P, FEATURES], F32)
             for head in range(HEADS):
-                nc.gpsimd.tensor_scalar(
+                nc.scalar.activation(
                     out=result[:, cols(head, HEAD_DIM)],
-                    in0=sums[:, cols(head, HEAD_DIM)],
-                    scalar1=inverse_sum[i][:, head : head + 1],
-                    scalar2=0.0,
-                    op0=ALU.mult,
-                    op1=ALU.add,
+                    in_=out_sum[i][:, cols(head, HEAD_DIM)],
+                    func=ACT.Copy,
+                    scale=inverse_sum[i][:, head : head + 1],
                 )
             nc.sync.dma_start(out=out[0, cols(i, P), :], in_=result[:])
 
@@ -471,21 +461,28 @@ def tile_gatlayer_pa_kernel(tc, q, k, h, w_v, adj, out):
                     group_weights(n - 3, half)
             if head == 0 and i + 1 < ROW_TILES:
                 keep_queries(i + 1)
+            if head == 2 and 2 <= i:
+                finish_rows(i - 2)
             if n < UNITS:
                 empty_bank(n, 0)
             if n - 1 < UNITS:
                 if n > 1:
                     row_minimum(n - 1)
                     exponentials(n - 1)
-            if head == 2 and 2 <= i:
-                finish_rows(i - 2)
             if n < UNITS:
                 empty_bank(n, 1)
             if n + 1 < UNITS:
-                score_first_pair(n + 1)
+                score_pair_matmuls(n + 1, FIRST_PAIR)
+            if n + 1 < UNITS:
+                score_pair_penalty(n + 1, FIRST_PAIR)
             if 0 <= n - 2 < UNITS:
-                for half in reversed(range(2)):
-                    flip_weights(n - 2, half)
+                flip_weights(n - 2, 1)
+            if 0 <= n - 2 < UNITS:
+                flip_weights(n - 2, 0)
+            if 0 <= n - 2 < NODE_PASSES:
+                quantise_v(n - 2)
+            if 0 <= n - 4 < UNITS:
+                quantise(n - 4)
             if head == 1 and next_edges:
                 keep_edges(i + 1, 0)
                 penalty_for_tensor(i + 1, 0)
@@ -494,10 +491,6 @@ def tile_gatlayer_pa_kernel(tc, q, k, h, w_v, adj, out):
                 keep_edges(i + 1, 4)
                 penalty_for_tensor(i + 1, 2)
                 penalty_for_tensor(i + 1, 3)
-            if 0 <= n - 2 < NODE_PASSES:
-                quantise_v(n - 2)
-            if 0 <= n - 4 < UNITS:
-                quantise(n - 4)
             if n < UNITS:
                 for c in SECOND_PAIR:
                     empty_bank(n, c)
@@ -506,19 +499,19 @@ def tile_gatlayer_pa_kernel(tc, q, k, h, w_v, adj, out):
                 multiply_h(2)
                 group_v(2)
             if n + 1 < UNITS:
-                penalty_of_second_pair(n + 1)
+                score_pair_matmuls(n + 1, SECOND_PAIR)
+            if 0 <= n - LAG < UNITS:
+                aggregate(n - LAG)
+                if n - LAG >= UNITS - HEADS:
+                    finish_head(ROW_TILES - 1, (n - LAG) % HEADS)
+            if n + 1 < UNITS:
+                score_pair_penalty(n + 1, SECOND_PAIR)
             if head == 0 and next_edges:
                 flip_edges(i + 1, 0)
             if head == 1 and next_edges:
                 flip_edges(i + 1, 4)
             if head == 3 and i + 2 < ROW_TILES:
                 flip_queries(i + 2)
-            if n + 1 < UNITS:
-                score_second_pair(n + 1)
-            if 0 <= n - LAG < UNITS:
-                aggregate(n - LAG)
-                if n - LAG >= UNITS - HEADS:
-                    finish_head(ROW_TILES - 1, (n - LAG) % HEADS)
             if n == 1:
                 multiply_h(3)
                 group_v(3)
@@ -537,15 +530,15 @@ def tile_gatlayer_pa_kernel(tc, q, k, h, w_v, adj, out):
             for u in range(2):
                 group_h(0, u)
             group_w()
-            score_first_pair(0)
-            score_second_pair(0)
+            score_pair(0, FIRST_PAIR)
+            score_pair(0, SECOND_PAIR)
             flip_h(1)
             for u in range(2):
                 group_h(1, u)
             for c in FIRST_PAIR:
                 empty_bank(0, c)
             quantise_w()
-            score_first_pair(1)
+            score_pair(1, FIRST_PAIR)
             for u in range(2):
                 quantise_h(0, u)
             flip_h(2)
@@ -553,7 +546,7 @@ def tile_gatlayer_pa_kernel(tc, q, k, h, w_v, adj, out):
                 group_h(2, u)
             for c in SECOND_PAIR:
                 empty_bank(0, c)
-            score_second_pair(1)
+            score_pair(1, SECOND_PAIR)
             for u in range(2):
                 quantise_h(1, u)
             flip_h(3)

@@ -32,7 +32,6 @@ SECOND_PAIR = (2, 3)
 EARLY_ROWS = 2
 CHUNKS = NODES // (2 * P)
 LAG = 6
-LATE = 3
 SCALE = 1.0 / math.sqrt(HEAD_DIM)
 HUGE = 3.0e38
 
@@ -381,7 +380,10 @@ def tile_gatlayer_pa_kernel(tc, q, k, h, w_v, adj, out):
 
         def flip_weights(unit, half):
             e_pairs = weights[unit][:].bitcast(F32)
-            e_flip = ps_flip.tile([P, BANK], F32, tag="flip")
+            if unit == UNITS - 2:
+                e_flip = ps_prod.tile([P, BANK], F32, tag="prod")
+            else:
+                e_flip = ps_flip.tile([P, BANK], F32, tag="flip")
             for t in range(BANK // P):
                 nc.tensor.transpose(
                     e_flip[:, cols(t, P)], e_pairs[:, cols((BANK // P) * half + t, P)], ident_f32[:]
@@ -400,17 +402,26 @@ def tile_gatlayer_pa_kernel(tc, q, k, h, w_v, adj, out):
             else:
                 nc.scalar.copy(out=out_ap, in_=in_ap)
 
-        def quantise(unit):
-            e_codes = codes.tile([P, NODE_PASSES * P], U32, align_bytes=64)
-            e_scales = codes.tile([P, NODE_PASSES * P], U8, align_bytes=64)
-            nc.vector.quantize_mx(out=e_codes[:].bitcast(FP8X4), scales=e_scales[:], in_=e_grouped[unit][:])
-            e_quantised[unit] = (e_codes, e_scales)
+        def quantise(unit, half=None):
+            if half is None or half == 0:
+                e_codes = codes.tile([P, NODE_PASSES * P], U32, align_bytes=64)
+                e_scales = codes.tile([P, NODE_PASSES * P], U8, align_bytes=64)
+                e_quantised[unit] = (e_codes, e_scales)
+            part = slice(0, NODE_PASSES * P) if half is None else cols(half, NODE_PASSES * P // 2)
+            nc.vector.quantize_mx(
+                out=e_quantised[unit][0][:, part].bitcast(FP8X4),
+                scales=e_quantised[unit][1][:, part],
+                in_=e_grouped[unit][:, PACK * part.start : PACK * part.stop],
+            )
 
         def aggregate(unit):
             i, head = divmod(unit, HEADS)
             e_codes, e_scales = e_quantised[unit]
             if head == 0:
-                o_bank = ps_out.tile([P, BANK], F32, tag="out")
+                if i == ROW_TILES - 1:
+                    o_bank = ps_prod.tile([P, BANK], F32, tag="prod")
+                else:
+                    o_bank = ps_out.tile([P, BANK], F32, tag="out")
                 out_sum[i] = o_bank
             for g in range(NODE_PASSES):
                 nc.tensor.matmul_mx(
@@ -439,24 +450,51 @@ def tile_gatlayer_pa_kernel(tc, q, k, h, w_v, adj, out):
                 )
             nc.sync.dma_start(out=out[0, cols(i, P), :], in_=result[:])
 
-        def finish_head(i, head):
-            result = rows.tile([P, HEAD_DIM], F32)
+        def finish_head(head):
+            i = ROW_TILES - 1
+            out_ap = last_result[:, cols(head, HEAD_DIM)]
+            in_ap = out_sum[i][:, cols(head, HEAD_DIM)]
+            factor = inverse_sum[i][:, head : head + 1]
+            if head == HEADS - 1:
+                nc.vector.tensor_scalar(out=out_ap, in0=in_ap, scalar1=factor, scalar2=None, op0=ALU.mult)
+            else:
+                nc.scalar.activation(out=out_ap, in_=in_ap, func=ACT.Copy, scale=factor)
+            nc.sync.dma_start(out=out[0, cols(i, P), cols(head, HEAD_DIM)], in_=out_ap)
+
+        half_sums = keep.tile([P, 2], F32)
+        last_result = keep.tile([P, FEATURES], F32)
+
+        def last_exponentials(half):
+            unit = UNITS - 1
+            if half == 0:
+                e = work.tile([P, NODES], BF16)
+                weights[unit] = e
             nc.scalar.activation(
-                out=result[:],
-                in_=out_sum[i][:, cols(head, HEAD_DIM)],
-                func=ACT.Copy,
-                scale=inverse_sum[i][:, head : head + 1],
+                out=weights[unit][:, cols(half, NODES // 2)],
+                in_=neg_scores[unit][:, cols(half, NODES // 2)],
+                func=ACT.Exp,
+                bias=neg_max[unit][:],
+                scale=-1.0,
+                accum_out=half_sums[:, half : half + 1],
             )
-            nc.sync.dma_start(out=out[0, cols(i, P), cols(head, HEAD_DIM)], in_=result[:])
+
+        def invert_last_row_sums():
+            total = rows.tile([P, 1], F32)
+            nc.vector.tensor_tensor(out=total[:], in0=half_sums[:, 0:1], in1=half_sums[:, 1:2], op=ALU.add)
+            inverse = rows.tile([P, HEADS], F32)
+            last = HEADS - 1
+            nc.vector.reciprocal(out=inverse[:, :last], in_=row_sum[ROW_TILES - 1][:, :last])
+            nc.vector.reciprocal(out=inverse[:, last:HEADS], in_=total[:])
+            inverse_sum[ROW_TILES - 1] = inverse
 
         def step(n):
             i, head = divmod(n, HEADS)
             next_edges = EARLY_ROWS <= i + 1 < ROW_TILES
             if head == 0 and i + 2 < ROW_TILES:
                 load_rows(i + 2)
-            if head == 2 and 1 <= i <= ROW_TILES:
+            if head == 2 and i >= 1:
                 invert_row_sums(i - 1)
-            if 0 <= n - 3 < UNITS - LATE:
+            if n >= 3:
                 for half in range(2):
                     group_weights(n - 3, half)
             if head == 0 and i + 1 < ROW_TILES:
@@ -466,9 +504,8 @@ def tile_gatlayer_pa_kernel(tc, q, k, h, w_v, adj, out):
             if n < UNITS:
                 empty_bank(n, 0)
             if n - 1 < UNITS:
-                if n > 1:
-                    row_minimum(n - 1)
-                    exponentials(n - 1)
+                row_minimum(n - 1)
+                exponentials(n - 1)
             if n < UNITS:
                 empty_bank(n, 1)
             if n + 1 < UNITS:
@@ -494,16 +531,10 @@ def tile_gatlayer_pa_kernel(tc, q, k, h, w_v, adj, out):
             if n < UNITS:
                 for c in SECOND_PAIR:
                     empty_bank(n, c)
-            if n == 1:
-                group_v(1)
-                multiply_h(2)
-                group_v(2)
             if n + 1 < UNITS:
                 score_pair_matmuls(n + 1, SECOND_PAIR)
             if 0 <= n - LAG < UNITS:
                 aggregate(n - LAG)
-                if n - LAG >= UNITS - HEADS:
-                    finish_head(ROW_TILES - 1, (n - LAG) % HEADS)
             if n + 1 < UNITS:
                 score_pair_penalty(n + 1, SECOND_PAIR)
             if head == 0 and next_edges:
@@ -512,64 +543,98 @@ def tile_gatlayer_pa_kernel(tc, q, k, h, w_v, adj, out):
                 flip_edges(i + 1, 4)
             if head == 3 and i + 2 < ROW_TILES:
                 flip_queries(i + 2)
-            if n == 1:
-                multiply_h(3)
-                group_v(3)
-                flip_keys(3)
-            if UNITS - LATE <= n - 3 < UNITS:
-                for half in range(2):
-                    group_weights(n - 3, half, by_vector=n - 3 < UNITS - 1 or half == 0)
 
-        def first_step():
+        def first_steps():
+            both = range(2)
             penalty_early(0)
             flip_queries(0)
             keep_queries(0)
             flip_keys(0)
             flip_keys(1)
-            flip_h(0)
-            for u in range(2):
-                group_h(0, u)
+            for g in both:
+                flip_h(g)
+                for u in both:
+                    group_h(g, u)
             group_w()
             score_pair(0, FIRST_PAIR)
+            flip_h(2)
+            for u in both:
+                group_h(2, u)
             score_pair(0, SECOND_PAIR)
-            flip_h(1)
-            for u in range(2):
-                group_h(1, u)
+            flip_h(3)
+            for u in both:
+                group_h(3, u)
             for c in FIRST_PAIR:
                 empty_bank(0, c)
             quantise_w()
-            score_pair(1, FIRST_PAIR)
-            for u in range(2):
+            for u in both:
                 quantise_h(0, u)
-            flip_h(2)
-            for u in range(2):
-                group_h(2, u)
+            score_pair(1, FIRST_PAIR)
             for c in SECOND_PAIR:
                 empty_bank(0, c)
-            score_pair(1, SECOND_PAIR)
-            for u in range(2):
+            for u in both:
                 quantise_h(1, u)
-            flip_h(3)
-            for u in range(2):
-                group_h(3, u)
             row_minimum(0)
+            multiply_h(0)
+            score_pair(1, SECOND_PAIR)
+            group_v(0)
             exponentials(0)
-            for g in range(2, NODE_PASSES):
-                for u in range(2):
-                    quantise_h(g, u)
+            for u in both:
+                quantise_h(2, u)
+            penalty_early(1)
+            flip_keys(2)
+            multiply_h(1)
+            for c in FIRST_PAIR:
+                empty_bank(1, c)
+            group_v(1)
+            score_pair(2, FIRST_PAIR)
+            for u in both:
+                quantise_h(3, u)
+            for c in SECOND_PAIR:
+                empty_bank(1, c)
+            multiply_h(2)
+            score_pair(2, SECOND_PAIR)
+            group_v(2)
+            multiply_h(3)
+            group_v(3)
             flip_queries(1)
             keep_queries(1)
-            flip_keys(2)
-            penalty_early(1)
-            multiply_h(0)
-            group_v(0)
-            multiply_h(1)
+            flip_keys(3)
             load_rows(2)
 
-        with tc.manual_schedule():
-            first_step()
-            for n in range(1, UNITS + 4):
-                step(n)
-            for unit in range(UNITS + 4 - LAG, UNITS):
+        def last_steps():
+            last = UNITS - 1
+            row_minimum(last)
+            for half in range(2):
+                last_exponentials(half)
+            for unit in range(last - 5, last - 3):
                 aggregate(unit)
-                finish_head(ROW_TILES - 1, unit % HEADS)
+            for half in range(2):
+                group_weights(last - 2, half, by_vector=True)
+            quantise(last - 3)
+            for half in range(2):
+                flip_weights(last - 1, half)
+            for half in range(2):
+                group_weights(last - 1, half, by_vector=True)
+            aggregate(last - 3)
+            for half in range(2):
+                flip_weights(last, half)
+            group_weights(last, 0, by_vector=True)
+            group_weights(last, 1)
+            finish_rows(ROW_TILES - 2)
+            quantise(last - 2)
+            aggregate(last - 2)
+            quantise(last, 0)
+            invert_last_row_sums()
+            quantise(last - 1)
+            aggregate(last - 1)
+            quantise(last, 1)
+            aggregate(last)
+            for head in range(HEADS):
+                finish_head(head)
+
+        with tc.manual_schedule():
+            first_steps()
+            for n in range(2, UNITS):
+                step(n)
+            last_steps()

@@ -337,6 +337,20 @@ def tile_gatlayer_pa_kernel(tc, q, k, h, w_v, adj, out):
             for c in reversed(pair):
                 add_penalty(unit, c, opens=False)
 
+        def open_second_pair(unit):
+            if unit < EARLY_ROWS * HEADS:
+                return
+            new_banks(unit, SECOND_PAIR)
+            for c in SECOND_PAIR:
+                add_penalty(unit, c, opens=True)
+
+        def close_second_pair(unit):
+            if unit < EARLY_ROWS * HEADS:
+                score_early(unit, SECOND_PAIR)
+                return
+            for c in reversed(SECOND_PAIR):
+                score_matmul(unit, c, opens=False)
+
         def score_pair(unit, pair):
             score_pair_matmuls(unit, pair)
             score_pair_penalty(unit, pair)
@@ -532,17 +546,17 @@ def tile_gatlayer_pa_kernel(tc, q, k, h, w_v, adj, out):
                 for c in SECOND_PAIR:
                     empty_bank(n, c)
             if n + 1 < UNITS:
-                score_pair_matmuls(n + 1, SECOND_PAIR)
-            if 0 <= n - LAG < UNITS:
-                aggregate(n - LAG)
-            if n + 1 < UNITS:
-                score_pair_penalty(n + 1, SECOND_PAIR)
+                open_second_pair(n + 1)
             if head == 0 and next_edges:
                 flip_edges(i + 1, 0)
             if head == 1 and next_edges:
                 flip_edges(i + 1, 4)
             if head == 3 and i + 2 < ROW_TILES:
                 flip_queries(i + 2)
+            if n + 1 < UNITS:
+                close_second_pair(n + 1)
+            if 0 <= n - LAG < UNITS:
+                aggregate(n - LAG)
 
         def first_steps():
             both = range(2)

@@ -240,7 +240,11 @@ def tile_gatlayer_pa_kernel(tc, q, k, h, w_v, adj, out):
             if first == 0:
                 flipped = rows.tile([P, CHUNKS * P], F32)
                 edges_flipped[i] = flipped
-            nc.vector.tensor_copy(out=edges_flipped[i][:, cols(first // 4, BANK)], in_=edges_in_psum[(i, first)][:])
+            out_ap = edges_flipped[i][:, cols(first // 4, BANK)]
+            if first == 0:
+                nc.vector.tensor_copy(out=out_ap, in_=edges_in_psum[(i, first)][:])
+            else:
+                nc.scalar.copy(out=out_ap, in_=edges_in_psum[(i, first)][:])
 
         def penalty_for_tensor(i, g):
             if g == 0:
@@ -455,13 +459,12 @@ def tile_gatlayer_pa_kernel(tc, q, k, h, w_v, adj, out):
 
         def finish_rows(i):
             result = rows.tile([P, FEATURES], F32)
-            for head in range(HEADS):
-                nc.scalar.activation(
-                    out=result[:, cols(head, HEAD_DIM)],
-                    in_=out_sum[i][:, cols(head, HEAD_DIM)],
-                    func=ACT.Copy,
-                    scale=inverse_sum[i][:, head : head + 1],
-                )
+            nc.vector.tensor_tensor(
+                out=result[:].rearrange("p (n d) -> p n d", d=HEAD_DIM),
+                in0=out_sum[i][:].rearrange("p (n d) -> p n d", d=HEAD_DIM),
+                in1=inverse_sum[i][:].unsqueeze(2).to_broadcast([P, HEADS, HEAD_DIM]),
+                op=ALU.mult,
+            )
             nc.sync.dma_start(out=out[0, cols(i, P), :], in_=result[:])
 
         def finish_head(head):
@@ -513,8 +516,6 @@ def tile_gatlayer_pa_kernel(tc, q, k, h, w_v, adj, out):
                     group_weights(n - 3, half)
             if head == 0 and i + 1 < ROW_TILES:
                 keep_queries(i + 1)
-            if head == 2 and 2 <= i:
-                finish_rows(i - 2)
             if n < UNITS:
                 empty_bank(n, 0)
             if n - 1 < UNITS:
@@ -534,6 +535,8 @@ def tile_gatlayer_pa_kernel(tc, q, k, h, w_v, adj, out):
                 quantise_v(n - 2)
             if 0 <= n - 4 < UNITS:
                 quantise(n - 4)
+            if head == 2 and 2 <= i:
+                finish_rows(i - 2)
             if head == 1 and next_edges:
                 keep_edges(i + 1, 0)
                 penalty_for_tensor(i + 1, 0)

import math
from contextlib import ExitStack

import concourse.mybir as mybir
from concourse.masks import make_identity

FLOPS = 2 * 2048 * 512 * 512 + 2 * (2 * 4 * 2048 * 2048 * 128)

FP8X4 = mybir.dt.float8_e4m3fn_x4
BF16 = mybir.dt.bfloat16
F32 = mybir.dt.float32
U32 = mybir.dt.uint32
U8 = mybir.dt.uint8
ALU = mybir.AluOpType
ACT = mybir.ActivationFunctionType
AXIS = mybir.AxisListType

P = 128
PACK = 4
K_PASS = P * PACK
BANK = 512
NODES = 2048
FEATURES = 512
HEADS = 4
HEAD_DIM = 128
ROW_TILES = NODES // P
UNITS = ROW_TILES * HEADS
SCORE_BANKS = NODES // BANK
NODE_PASSES = NODES // K_PASS
FIRST_PAIR = (0, 1)
SECOND_PAIR = (2, 3)
EARLY_ROWS = 2
CHUNKS = NODES // (2 * P)
LAG = 6
SCALE = 1.0 / math.sqrt(HEAD_DIM)
HUGE = 3.0e38


def cols(index, width):
    return slice(index * width, (index + 1) * width)


def tile_gatlayer_pa_kernel(tc, q, k, h, w_v, adj, out):
    nc = tc.nc
    with ExitStack() as ctx:
        const = ctx.enter_context(tc.tile_pool(name="const", bufs=1))
        keep = ctx.enter_context(tc.tile_pool(name="keep", bufs=1))
        stage = ctx.enter_context(tc.tile_pool(name="stage", bufs=4))
        rows = ctx.enter_context(tc.tile_pool(name="rows", bufs=2))
        work = ctx.enter_context(tc.tile_pool(name="work", bufs=3))
        codes = ctx.enter_context(tc.tile_pool(name="codes", bufs=LAG))
        ps_prod = ctx.enter_context(tc.psum_pool(name="ps_prod", bufs=4))
        ps_flip = ctx.enter_context(tc.psum_pool(name="ps_flip", bufs=2))
        ps_out = ctx.enter_context(tc.psum_pool(name="ps_out", bufs=1))
        ps_misc = ctx.enter_context(tc.psum_pool(name="ps_misc", bufs=1))

        ident_f32 = const.tile([P, P], F32)
        make_identity(nc, ident_f32[:])
        ident_bf16 = const.tile([P, P], BF16)
        make_identity(nc, ident_bf16[:])

        def grouped_view(grouped):
            return grouped.rearrange("p (c t) -> p c t", t=PACK)

        q_rows = {}
        adj_rows = {}

        def load_rows(i):
            adj_tile = rows.tile([P, NODES], BF16)
            nc.sync.dma_start(out=adj_tile[:], in_=adj[cols(i, P), :])
            adj_rows[i] = adj_tile
            q_tile = rows.tile([P, HEADS, HEAD_DIM], BF16)
            nc.sync.dma_start(out=q_tile[:], in_=q[0, :, cols(i, P), :].rearrange("n p d -> p n d"))
            q_rows[i] = q_tile

        k_rows = keep.tile([P, HEADS, ROW_TILES // 2, 2, HEAD_DIM], BF16)

        def load_keys(head):
            nc.sync.dma_start(
                out=k_rows[:, head, :, :, :], in_=k[0, head].rearrange("(m p b) d -> p m b d", p=P, b=2)
            )

        load_rows(0)
        load_keys(0)
        load_keys(1)
        w_rows = keep.tile([P, PACK, FEATURES], BF16)
        nc.sync.dma_start(
            out=w_rows[:].rearrange("p (u b) c -> p u b c", u=2),
            in_=w_v.rearrange("(u p b) c -> p u b c", u=2, b=2),
        )
        h_rows = keep.tile([P, NODE_PASSES, PACK, FEATURES], BF16)

        def load_features(g):
            nc.sync.dma_start(
                out=h_rows[:, g, :, :], in_=h[0, cols(g, K_PASS), :].rearrange("(p s) k -> p s k", s=PACK)
            )

        for g in range(NODE_PASSES):
            load_features(g)
        load_keys(2)
        load_rows(1)
        load_keys(3)

        w_codes = keep.tile([P, FEATURES], U32, align_bytes=64)
        w_scales = keep.tile([P, FEATURES], U8, align_bytes=64)
        h_codes = keep.tile([P, NODES], U32, align_bytes=64)
        h_scales = keep.tile([P, NODES], U8, align_bytes=64)
        v_codes = keep.tile([P, NODE_PASSES, FEATURES], U32, align_bytes=64)
        v_scales = keep.tile([P, NODE_PASSES, FEATURES], U8, align_bytes=64)

        v_grouped = keep.tile([P, NODE_PASSES, FEATURES * PACK], BF16, align_bytes=64)

        def shared_copy(piece, out_ap, in_ap):
            if piece % 2 == 1:
                nc.vector.tensor_copy(out=out_ap, in_=in_ap)
            else:
                nc.scalar.copy(out=out_ap, in_=in_ap)

        w_grouped = keep.tile([P, FEATURES * PACK], BF16, align_bytes=64)

        def group_w():
            nc.vector.tensor_copy(out=grouped_view(w_grouped[:]), in_=w_rows[:].rearrange("p t c -> p c t"))

        def quantise_w():
            nc.vector.quantize_mx(out=w_codes[:].bitcast(FP8X4), scales=w_scales[:], in_=w_grouped[:])

        h_flipped = {}
        h_grouped = {}

        def flip_h(g):
            for u in range(2):
                h_flip = spare_bank(2 * (g % 2) + u, F32)
                for b in range(2):
                    h_pairs = h_rows[:, g, 2 * b + u, :].bitcast(F32)
                    for v in range(2):
                        nc.tensor.transpose(h_flip[:, cols(2 * b + v, P)], h_pairs[:, cols(v, P)], ident_f32[:])
                h_flipped[(g, u)] = h_flip

        def group_h(g, u):
            grouped = stage.tile([P, 2 * P * PACK], BF16, align_bytes=64)
            nc.scalar.copy(
                out=grouped[:].bitcast(F32).rearrange("p (b r v) -> p b r v", b=2, v=2),
                in_=h_flipped[(g, u)][:].rearrange("p (b v r) -> p b r v", b=2, v=2),
            )
            h_grouped[(g, u)] = grouped

        def quantise_h(g, u):
            a = 2 * g + u
            nc.vector.quantize_mx(
                out=h_codes[:, cols(a, 2 * P)].bitcast(FP8X4),
                scales=h_scales[:, cols(a, 2 * P)],
                in_=h_grouped[(g, u)][:],
            )

        v_sums = {}

        def multiply_h(g):
            for t in range(PACK):
                v_sum = spare_bank(t, F32)
                v_sums[(g, t)] = v_sum
                nc.tensor.matmul_mx(
                    out=v_sum[:],
                    lhsT=h_codes[:, cols(PACK * g + t, P)].bitcast(FP8X4),
                    lhsT_scale=h_scales[:, cols(PACK * g + t, P)],
                    rhs=w_codes[:].bitcast(FP8X4),
                    rhs_scale=w_scales[:],
                    start=True,
                    stop=True,
                )

        def group_v(g):
            v_rows = stage.tile([P, PACK, FEATURES], BF16)
            for t in range(PACK):
                shared_copy(1 if t == 3 else 0, v_rows[:, t, :], v_sums[(g, t)][:])
            nc.gpsimd.tensor_scalar(
                out=grouped_view(v_grouped[:, g, :]),
                in0=v_rows[:].rearrange("p t c -> p c t"),
                scalar1=1.0,
                scalar2=0.0,
                op0=ALU.mult,
                op1=ALU.add,
            )

        def quantise_v(g):
            nc.vector.quantize_mx(
                out=v_codes[:, g, :].bitcast(FP8X4), scales=v_scales[:, g, :], in_=v_grouped[:, g, :]
            )

        k_flipped = keep.tile([P, HEADS, NODES], BF16)

        def copy_flipped(by_vector, out_ap, in_ap):
            if by_vector:
                nc.vector.tensor_copy(out=out_ap, in_=in_ap)
            else:
                nc.scalar.copy(out=out_ap, in_=in_ap)

        def spare_bank(place, dtype):
            if place == 2:
                bank = ps_out.tile([P, BANK], dtype, tag="out")
            elif place == 3:
                bank = ps_misc.tile([P, BANK], dtype, tag="misc")
            else:
                bank = ps_flip.tile([P, BANK], dtype, tag="flip")
            return bank

        def flip_keys(head):
            for c in range(SCORE_BANKS):
                k_flip = spare_bank(c if head < 3 else 0, BF16)
                for t in range(BANK // P):
                    b, m = divmod(t, 2)
                    nc.tensor.transpose(k_flip[:, cols(t, P)], k_rows[:, head, 2 * c + m, b, :], ident_bf16[:])
                copy_flipped(head == 2 or (c % 2 == 0 and head < 2), k_flipped[:, head, cols(c, BANK)], k_flip[:])

        edges_in_psum = {}
        edges_flipped = {}
        penalty_t = {}
        penalty_n = {}
        minima = {}
        q_in_psum = {}
        q_flipped = {}
        inverse_sum = {}
        row_sum = {}
        out_sum = {}
        scores = {}
        neg_scores = {}
        neg_max = {}
        weights = {}
        e_flipped = {}
        e_grouped = {}
        e_quantised = {}

        def flip_edges(i, first):
            words = adj_rows[i][:].bitcast(F32)
            bank = ps_misc.tile([P, BANK], F32, tag="misc")
            for c in range(first, first + 4):
                nc.tensor.transpose(bank[:, cols(c - first, P)], words[:, cols(c, P)], ident_f32[:])
            edges_in_psum[(i, first)] = bank

        def keep_edges(i, first):
            if first == 0:
                flipped = rows.tile([P, CHUNKS * P], F32)
                edges_flipped[i] = flipped
            out_ap = edges_flipped[i][:, cols(first // 4, BANK)]
            if first == 0:
                nc.vector.tensor_copy(out=out_ap, in_=edges_in_psum[(i, first)][:])
            else:
                nc.scalar.copy(out=out_ap, in_=edges_in_psum[(i, first)][:])

        def penalty_for_tensor(i, g):
            if g == 0:
                pen = rows.tile([P, SCORE_BANKS, 2, 2, P], F32)
                penalty_t[i] = pen
            edges = edges_flipped[i][:].bitcast(BF16)[:, cols(g, 4 * P)]
            nc.gpsimd.tensor_scalar(
                out=penalty_t[i][:, g, :, :, :],
                in0=edges.rearrange("p (m i b) -> p m b i", m=2, b=2),
                scalar1=HUGE,
                scalar2=-HUGE,
                op0=ALU.mult,
                op1=ALU.add,
            )

        def penalty_early(i):
            pen = rows.tile([P, NODES], BF16)
            for g in range(SCORE_BANKS):
                nc.gpsimd.tensor_scalar(
                    out=pen[:, cols(g, BANK)].rearrange("p (b y) -> p b y", b=2),
                    in0=adj_rows[i][:, cols(g, BANK)].rearrange("p (y b) -> p b y", b=2),
                    scalar1=HUGE,
                    scalar2=-HUGE,
                    op0=ALU.mult,
                    op1=ALU.add,
                )
            penalty_n[i] = pen

        def flip_queries(i):
            q_flip = ps_misc.tile([P, BANK], BF16, tag="misc")
            for head in range(HEADS):
                nc.tensor.transpose(q_flip[:, cols(head, P)], q_rows[i][:, head, :], ident_bf16[:])
            q_in_psum[i] = q_flip

        def keep_queries(i):
            q_t = rows.tile([P, HEADS * P], BF16)
            copy_flipped(i == 0, q_t[:], q_in_psum[i][:])
            q_flipped[i] = q_t

        def score_matmul(unit, c, opens):
            i, head = divmod(unit, HEADS)
            nc.tensor.matmul(
                out=scores[(unit, c)][:],
                lhsT=q_flipped[i][:, cols(head, P)],
                rhs=k_flipped[:, head, cols(c, BANK)],
                start=opens,
                stop=not opens,
            )

        def add_penalty(unit, c, opens):
            i = unit // HEADS
            for t in range(BANK // P):
                b, m = divmod(t, 2)
                nc.tensor.matmul(
                    out=scores[(unit, c)][:, cols(t, P)],
                    lhsT=penalty_t[i][:, c, m, b, :],
                    rhs=ident_f32[:],
                    start=opens and t == 0,
                    stop=not opens and t == BANK // P - 1,
                    is_transpose=True,
                )

        def add_penalty_early(unit, c):
            nc.tensor.matmul(
                out=scores[(unit, c)][:],
                lhsT=ident_bf16[:],
                rhs=penalty_n[unit // HEADS][:, cols(c, BANK)],
                start=False,
                stop=True,
            )

        def score_early(unit, pair):
            new_banks(unit, pair)
            for c in reversed(pair):
                score_matmul(unit, c, opens=True)
                add_penalty_early(unit, c)

        def new_banks(unit, pair):
            for c in pair:
                s_bank = ps_prod.tile([P, BANK], F32, tag="prod")
                scores[(unit, c)] = s_bank

        def score_pair_matmuls(unit, pair):
            if unit < EARLY_ROWS * HEADS:
                score_early(unit, pair)
                return
            new_banks(unit, pair)
            for c in pair:
                score_matmul(unit, c, opens=True)

        def score_pair_penalty(unit, pair):
            if unit < EARLY_ROWS * HEADS:
                return
            for c in reversed(pair):
                add_penalty(unit, c, opens=False)

        def open_second_pair(unit):
            if unit < EARLY_ROWS * HEADS:
                return
            new_banks(unit, SECOND_PAIR)
            for c in SECOND_PAIR:
                add_penalty(unit, c, opens=True)

        def close_second_pair(unit):
            if unit < EARLY_ROWS * HEADS:
                score_early(unit, SECOND_PAIR)
                return
            for c in reversed(SECOND_PAIR):
                score_matmul(unit, c, opens=False)

        def score_pair(unit, pair):
            score_pair_matmuls(unit, pair)
            score_pair_penalty(unit, pair)

        def empty_bank(unit, c):
            if c == 0:
                x = work.tile([P, NODES], F32)
                neg_scores[unit] = x
                mins = work.tile([P, SCORE_BANKS], F32)
                minima[unit] = mins
            nc.vector.tensor_scalar(
                out=neg_scores[unit][:, cols(c, BANK)],
                in0=scores[(unit, c)][:],
                scalar1=-SCALE,
                scalar2=None,
                op0=ALU.mult,
                op1=ALU.min,
                accum_out=minima[unit][:, c : c + 1],
            )

        def row_minimum(unit):
            x_min = work.tile([P, 1], F32)
            nc.vector.tensor_reduce(out=x_min[:], in_=minima[unit][:], axis=AXIS.X, op=ALU.min)
            neg_max[unit] = x_min

        def exponentials(unit):
            i, head = divmod(unit, HEADS)
            if head == 0:
                sums = rows.tile([P, HEADS], F32)
                row_sum[i] = sums
            e = work.tile([P, NODES], BF16)
            nc.scalar.activation(
                out=e[:],
                in_=neg_scores[unit][:],
                func=ACT.Exp,
                bias=neg_max[unit][:],
                scale=-1.0,
                accum_out=row_sum[i][:, head : head + 1],
            )
            weights[unit] = e

        def flip_weights(unit, half):
            e_pairs = weights[unit][:].bitcast(F32)
            if unit == UNITS - 2:
                e_flip = ps_prod.tile([P, BANK], F32, tag="prod")
            else:
                e_flip = ps_flip.tile([P, BANK], F32, tag="flip")
            for t in range(BANK // P):
                nc.tensor.transpose(
                    e_flip[:, cols(t, P)], e_pairs[:, cols((BANK // P) * half + t, P)], ident_f32[:]
                )
            e_flipped[(unit, half)] = e_flip

        def group_weights(unit, half, by_vector=False):
            if half == 0:
                grouped = work.tile([P, NODE_PASSES * P * PACK], BF16, align_bytes=64)
                e_grouped[unit] = grouped
            grouped_pairs = e_grouped[unit][:].bitcast(F32).rearrange("p (g r u) -> p g r u", r=P, u=2)
            out_ap = grouped_pairs[:, cols(half, 2), :, :]
            in_ap = e_flipped[(unit, half)][:].rearrange("p (g u r) -> p g r u", g=2, u=2)
            if by_vector:
                nc.vector.tensor_copy(out=out_ap, in_=in_ap)
            else:
                nc.scalar.copy(out=out_ap, in_=in_ap)

        def quantise(unit, half=None):
            if half is None or half == 0:
                e_codes = codes.tile([P, NODE_PASSES * P], U32, align_bytes=64)
                e_scales = codes.tile([P, NODE_PASSES * P], U8, align_bytes=64)
                e_quantised[unit] = (e_codes, e_scales)
            part = slice(0, NODE_PASSES * P) if half is None else cols(half, NODE_PASSES * P // 2)
            nc.vector.quantize_mx(
                out=e_quantised[unit][0][:, part].bitcast(FP8X4),
                scales=e_quantised[unit][1][:, part],
                in_=e_grouped[unit][:, PACK * part.start : PACK * part.stop],
            )

        def aggregate(unit):
            i, head = divmod(unit, HEADS)
            e_codes, e_scales = e_quantised[unit]
            if head == 0:
                if i == ROW_TILES - 1:
                    o_bank = ps_prod.tile([P, BANK], F32, tag="prod")
                else:
                    o_bank = ps_out.tile([P, BANK], F32, tag="out")
                out_sum[i] = o_bank
            for g in range(NODE_PASSES):
                nc.tensor.matmul_mx(
                    out=out_sum[i][:, cols(head, HEAD_DIM)],
                    lhsT=e_codes[:, cols(g, P)].bitcast(FP8X4),
                    lhsT_scale=e_scales[:, cols(g, P)],
                    rhs=v_codes[:, g, cols(head, HEAD_DIM)].bitcast(FP8X4),
                    rhs_scale=v_scales[:, g, cols(head, HEAD_DIM)],
                    start=(g == 0),
                    stop=(g == NODE_PASSES - 1),
                )

        def invert_row_sums(i):
            inverse = rows.tile([P, HEADS], F32)
            nc.vector.reciprocal(out=inverse[:], in_=row_sum[i][:])
            inverse_sum[i] = inverse

        def finish_rows(i):
            result = rows.tile([P, FEATURES], F32)
            nc.vector.tensor_tensor(
                out=result[:].rearrange("p (n d) -> p n d", d=HEAD_DIM),
                in0=out_sum[i][:].rearrange("p (n d) -> p n d", d=HEAD_DIM),
                in1=inverse_sum[i][:].unsqueeze(2).to_broadcast([P, HEADS, HEAD_DIM]),
                op=ALU.mult,
            )
            nc.sync.dma_start(out=out[0, cols(i, P), :], in_=result[:])

        def finish_head(head):
            i = ROW_TILES - 1
            out_ap = last_result[:, cols(head, HEAD_DIM)]
            in_ap = out_sum[i][:, cols(head, HEAD_DIM)]
            factor = inverse_sum[i][:, head : head + 1]
            if head == HEADS - 1:
                nc.vector.tensor_scalar(out=out_ap, in0=in_ap, scalar1=factor, scalar2=None, op0=ALU.mult)
            else:
                nc.scalar.activation(out=out_ap, in_=in_ap, func=ACT.Copy, scale=factor)
            nc.sync.dma_start(out=out[0, cols(i, P), cols(head, HEAD_DIM)], in_=out_ap)

        half_sums = keep.tile([P, 2], F32)
        last_result = keep.tile([P, FEATURES], F32)

        def last_exponentials(half):
            unit = UNITS - 1
            if half == 0:
                e = work.tile([P, NODES], BF16)
                weights[unit] = e
            nc.scalar.activation(
                out=weights[unit][:, cols(half, NODES // 2)],
                in_=neg_scores[unit][:, cols(half, NODES // 2)],
                func=ACT.Exp,
                bias=neg_max[unit][:],
                scale=-1.0,
                accum_out=half_sums[:, half : half + 1],
            )

        def invert_last_row_sums():
            total = rows.tile([P, 1], F32)
            nc.vector.tensor_tensor(out=total[:], in0=half_sums[:, 0:1], in1=half_sums[:, 1:2], op=ALU.add)
            inverse = rows.tile([P, HEADS], F32)
            last = HEADS - 1
            nc.vector.reciprocal(out=inverse[:, :last], in_=row_sum[ROW_TILES - 1][:, :last])
            nc.vector.reciprocal(out=inverse[:, last:HEADS], in_=total[:])
            inverse_sum[ROW_TILES - 1] = inverse

        def step(n):
            i, head = divmod(n, HEADS)
            next_edges = EARLY_ROWS <= i + 1 < ROW_TILES
            if head == 0 and i + 2 < ROW_TILES:
                load_rows(i + 2)
            if head == 2 and i >= 1:
                invert_row_sums(i - 1)
            if n >= 3:
                for half in range(2):
                    group_weights(n - 3, half)
            if head == 0 and i + 1 < ROW_TILES:
                keep_queries(i + 1)
            if n < UNITS:
                empty_bank(n, 0)
            if n - 1 < UNITS:
                row_minimum(n - 1)
                exponentials(n - 1)
            if n < UNITS:
                empty_bank(n, 1)
            if n + 1 < UNITS:
                score_pair_matmuls(n + 1, FIRST_PAIR)
            if n + 1 < UNITS:
                score_pair_penalty(n + 1, FIRST_PAIR)
            if 0 <= n - 2 < UNITS:
                flip_weights(n - 2, 1)
            if 0 <= n - 2 < UNITS:
                flip_weights(n - 2, 0)
            if 0 <= n - 2 < NODE_PASSES:
                quantise_v(n - 2)
            if 0 <= n - 4 < UNITS:
                quantise(n - 4)
            if head == 2 and 2 <= i:
                finish_rows(i - 2)
            if head == 1 and next_edges:
                keep_edges(i + 1, 0)
                penalty_for_tensor(i + 1, 0)
                penalty_for_tensor(i + 1, 1)
            if head == 2 and next_edges:
                keep_edges(i + 1, 4)
                penalty_for_tensor(i + 1, 2)
                penalty_for_tensor(i + 1, 3)
            if n < UNITS:
                for c in SECOND_PAIR:
                    empty_bank(n, c)
            if n + 1 < UNITS:
                open_second_pair(n + 1)
            if head == 0 and next_edges:
                flip_edges(i + 1, 0)
            if head == 1 and next_edges:
                flip_edges(i + 1, 4)
            if head == 3 and i + 2 < ROW_TILES:
                flip_queries(i + 2)
            if n + 1 < UNITS:
                close_second_pair(n + 1)
            if 0 <= n - LAG < UNITS:
                aggregate(n - LAG)

        def first_steps():
            both = range(2)
            penalty_early(0)
            flip_queries(0)
            keep_queries(0)
            flip_keys(0)
            flip_keys(1)
            for g in both:
                flip_h(g)
                for u in both:
                    group_h(g, u)
            group_w()
            score_pair(0, FIRST_PAIR)
            flip_h(2)
            for u in both:
                group_h(2, u)
            score_pair(0, SECOND_PAIR)
            flip_h(3)
            for u in both:
                group_h(3, u)
            for c in FIRST_PAIR:
                empty_bank(0, c)
            quantise_w()
            for u in both:
                quantise_h(0, u)
            score_pair(1, FIRST_PAIR)
            for c in SECOND_PAIR:
                empty_bank(0, c)
            for u in both:
                quantise_h(1, u)
            row_minimum(0)
            multiply_h(0)
            score_pair(1, SECOND_PAIR)
            group_v(0)
            exponentials(0)
            for u in both:
                quantise_h(2, u)
            penalty_early(1)
            flip_keys(2)
            multiply_h(1)
            for c in FIRST_PAIR:
                empty_bank(1, c)
            group_v(1)
            score_pair(2, FIRST_PAIR)
            for u in both:
                quantise_h(3, u)
            for c in SECOND_PAIR:
                empty_bank(1, c)
            multiply_h(2)
            score_pair(2, SECOND_PAIR)
            group_v(2)
            multiply_h(3)
            group_v(3)
            flip_queries(1)
            keep_queries(1)
            flip_keys(3)
            load_rows(2)

        def last_steps():
            last = UNITS - 1
            row_minimum(last)
            for half in range(2):
                last_exponentials(half)
            for unit in range(last - 5, last - 3):
                aggregate(unit)
            for half in range(2):
                group_weights(last - 2, half, by_vector=True)
            quantise(last - 3)
            for half in range(2):
                flip_weights(last - 1, half)
            for half in range(2):
                group_weights(last - 1, half, by_vector=True)
            aggregate(last - 3)
            for half in range(2):
                flip_weights(last, half)
            group_weights(last, 0, by_vector=True)
            group_weights(last, 1)
            finish_rows(ROW_TILES - 2)
            quantise(last - 2)
            aggregate(last - 2)
            quantise(last, 0)
            invert_last_row_sums()
            quantise(last - 1)
            aggregate(last - 1)
            quantise(last, 1)
            aggregate(last)
            for head in range(HEADS):
                finish_head(head)

        with tc.manual_schedule():
            first_steps()
            for n in range(2, UNITS):
                step(n)
            last_steps()
